import numpy as np
import ml_dtypes


def mxq(x, axis, fmt="e4m3"):
    dtype, down = {"e4m3": (ml_dtypes.float8_e4m3fn, 7), "e5m2": (ml_dtypes.float8_e5m2, 14)}[fmt]
    v = np.moveaxis(np.asarray(x, np.float32).astype(ml_dtypes.bfloat16).astype(np.float64), axis, -1)
    blocks = v.reshape(v.shape[:-1] + (-1, 32))
    amax = np.abs(blocks).max(-1, keepdims=True)
    byte = np.maximum(np.where(amax > 0, np.frexp(amax)[1] - 1 + 127, 0) - down, 1)
    scale = np.exp2(byte - 127.0)
    codes = (blocks / scale).astype(np.float32).astype(dtype).astype(np.float64)
    return np.moveaxis((codes * scale).reshape(v.shape), -1, axis)


WIDE = False


def mx_kscale(k):
    if not WIDE:
        return np.ones(k)
    levels = np.array([10, -10, 5, -5, 0])
    a = np.random.permutation(np.resize(levels, k // 512 * 4)).reshape(k // 512, 4)
    idx = np.arange(k)
    return np.exp2(a[idx // 512, idx % 128 // 32])


BF16 = ml_dtypes.bfloat16


def bf(x):
    return np.asarray(x, np.float32).astype(BF16)


def f64(x):
    return np.asarray(x).astype(np.float64)


N, D, N_BRANCH, N_OUT = 256, 1024, 512, 512
BLOCK = N_BRANCH // 4


def erf(v):
    a = np.minimum(np.abs(v), 6.0)
    term = a.copy()
    total = a.copy()
    for n in range(1, 120):
        term = term * (2.0 * a * a) / (2 * n + 1)
        total = total + term
    return np.sign(v) * 2.0 / np.sqrt(np.pi) * np.exp(-a * a) * total


def _branch_activations(h):
    return np.concatenate([
        np.maximum(h[:, 0 * BLOCK:1 * BLOCK], 0.0),
        np.tanh(h[:, 1 * BLOCK:2 * BLOCK]),
        1.0 / (1.0 + np.exp(-h[:, 2 * BLOCK:3 * BLOCK])),
        0.5 * h[:, 3 * BLOCK:4 * BLOCK] * (1.0 + erf(h[:, 3 * BLOCK:4 * BLOCK] / np.sqrt(2.0))),
    ], axis=-1)


def setup_inputs():
    s = mx_kscale(D)
    t = np.ones(N_BRANCH)
    t[:BLOCK] = mx_kscale(N_BRANCH)[:BLOCK]
    return {"x": bf(np.random.standard_normal((N, D)) * s),
            "W": bf(np.random.standard_normal((D, N_BRANCH)) * 1.0 / np.sqrt(D) / s[:, None] * t),
            "b": bf(np.random.standard_normal(N_BRANCH) * 0.3 * t),
            "agg": bf(np.random.standard_normal((N_BRANCH, N_OUT)) * 1.5 / np.sqrt(N_BRANCH) / t[:, None])}


def reference(x, W, b, agg):
    h = (mxq(f64(x), 1, "e4m3") @ mxq(f64(W), 0, "e4m3")) + f64(b)
    concatenated = _branch_activations(h)
    return mxq(concatenated, 1, "e4m3") @ mxq(f64(agg), 0, "e4m3")

@@ -1,0 +1,196 @@
+from concourse import mybir
+from concourse.masks import make_identity
+
+F32 = mybir.dt.float32
+BF16 = mybir.dt.bfloat16
+U32 = mybir.dt.uint32
+U8 = mybir.dt.uint8
+FP8X4 = mybir.dt.float8_e4m3fn_x4
+ACT = mybir.ActivationFunctionType
+ALU = mybir.AluOpType
+
+P = 128
+PACK = 4
+K_PASS = P * PACK
+
+TOKENS = 256
+D_IN = 1024
+BRANCHES = 512
+D_OUT = 512
+TOKEN_TILES = TOKENS // P
+D_PASSES = D_IN // K_PASS
+QUADRANT = 32
+
+FLOPS = 2 * TOKENS * D_IN * BRANCHES + 2 * TOKENS * BRANCHES * D_OUT
+
+W_VECTOR_M = 96
+AGG_VECTOR_COLS = 256
+
+
+def tile_kan_s_kernel(tc, x, W, b, agg, out):
+    nc = tc.nc
+    with tc.tile_pool(name="keep", bufs=1) as keep, tc.psum_pool(name="psum", bufs=1) as psum:
+        ident = keep.tile([P, P], F32)
+        make_identity(nc, ident[:])
+        slope = keep.tile([P, 1], F32)
+        offset = keep.tile([P, 1], F32)
+        nc.vector.memset(slope[:], 1.0)
+        nc.vector.memset(slope[2 * QUADRANT : 3 * QUADRANT, :], 0.5)
+        nc.vector.memset(offset[:], 0.0)
+        nc.vector.memset(offset[2 * QUADRANT : 3 * QUADRANT, :], 0.5)
+        warm = keep.tile([P, 1], F32)
+        nc.scalar.activation(out=warm[:], in_=offset[:], func=ACT.Gelu)
+
+        x_sb = []
+        for i in range(TOKEN_TILES):
+            x_tile = keep.tile([P, D_IN], BF16, name="x_sb%d" % i)
+            nc.sync.dma_start(out=x_tile[:], in_=x[i * P : (i + 1) * P, :])
+            x_sb.append(x_tile)
+        w_raw = keep.tile([P, D_PASSES, PACK, BRANCHES], BF16)
+        for g in range(D_PASSES):
+            nc.sync.dma_start(
+                out=w_raw[:, g, :, :].rearrange("p (u e) c -> p u (e c)", e=2),
+                in_=W[g * K_PASS : (g + 1) * K_PASS, :].rearrange("(u p e) c -> p u (e c)", u=2, e=2),
+            )
+        agg_raw = keep.tile([P, PACK, D_OUT], BF16)
+        nc.sync.dma_start(out=agg_raw[:], in_=agg.rearrange("(p t) o -> p t o", t=PACK))
+        b_sb = keep.tile([P, PACK], BF16)
+        nc.scalar.dma_start(out=b_sb[:], in_=b.rearrange("(p r) -> p r", r=PACK))
+
+        bias = keep.tile([P, PACK], F32)
+        nc.vector.tensor_copy(out=bias[:], in_=b_sb[:])
+        tanh_bias = keep.tile([P, PACK], F32)
+        nc.vector.tensor_scalar(
+            out=tanh_bias[:], in0=b_sb[:], scalar1=slope[:, 0:1], scalar2=None, op0=ALU.mult
+        )
+
+        x_grp = keep.tile([P, D_PASSES * TOKENS * PACK], BF16, align_bytes=64)
+        x_grp_words = x_grp[:].bitcast(F32).rearrange("p (g n u) -> p g n u", g=D_PASSES, u=2)
+        for i in range(TOKEN_TILES):
+            x_words = x_sb[i][:].bitcast(F32)
+            xt = psum.tile([P, D_PASSES, 2, P], F32, name="xt%d" % i)
+            for g in range(D_PASSES):
+                for u in range(2):
+                    first = (2 * g + u) * P
+                    nc.tensor.transpose(xt[:, g, u, :], x_words[:, first : first + P], ident[:])
+            nc.scalar.copy(
+                out=x_grp_words[:, :, i * P : (i + 1) * P, :],
+                in_=xt[:].rearrange("p g u n -> p g n u"),
+            )
+        x_codes = keep.tile([P, D_PASSES, TOKENS], U32, align_bytes=64)
+        x_scales = keep.tile([P, D_PASSES, TOKENS], U8, align_bytes=64)
+
+        w_grp = keep.tile([P, D_PASSES, PACK, P, PACK], BF16, align_bytes=64)
+        w_codes = keep.tile([P, D_PASSES, BRANCHES], U32, align_bytes=64)
+        w_scales = keep.tile([P, D_PASSES, BRANCHES], U8, align_bytes=64)
+
+        def regroup_w(g):
+            src = w_raw[:, g, :, :].rearrange("p t (m r) -> p m t r", r=PACK)
+            dst = w_grp[:, g, :, :, :].rearrange("p r m t -> p m t r")
+            nc.vector.tensor_copy(out=dst[:, :W_VECTOR_M], in_=src[:, :W_VECTOR_M])
+            nc.scalar.copy(out=dst[:, W_VECTOR_M:], in_=src[:, W_VECTOR_M:])
+
+        def quantise_w(g):
+            nc.vector.quantize_mx(
+                out=w_codes[:, g, :].bitcast(FP8X4),
+                scales=w_scales[:, g, :],
+                in_=w_grp[:, g, :, :, :].rearrange("p r m t -> p (r m t)"),
+            )
+
+        def quantise_x(g):
+            width = TOKENS * PACK
+            nc.vector.quantize_mx(
+                out=x_codes[:, g, :].bitcast(FP8X4),
+                scales=x_scales[:, g, :],
+                in_=x_grp[:, g * width : (g + 1) * width],
+            )
+
+        h_ps = [psum.tile([P, TOKENS], F32, name="h_ps%d" % r) for r in range(PACK)]
+
+        def first_product(g):
+            for r in range(PACK):
+                cols = slice(r * P, (r + 1) * P)
+                nc.tensor.matmul_mx(
+                    out=h_ps[r][:],
+                    lhsT=w_codes[:, g, cols].bitcast(FP8X4),
+                    lhsT_scale=w_scales[:, g, cols],
+                    rhs=x_codes[:, g, :].bitcast(FP8X4),
+                    rhs_scale=x_scales[:, g, :],
+                    start=(g == 0),
+                    stop=(g == D_PASSES - 1),
+                )
+
+        regroup_w(0)
+        quantise_x(0)
+        quantise_x(1)
+        quantise_w(0)
+        first_product(0)
+        regroup_w(1)
+        quantise_w(1)
+        first_product(1)
+
+        agg_grp = keep.tile([P, D_OUT, PACK], BF16, align_bytes=64)
+        agg_codes = keep.tile([P, D_OUT], U32, align_bytes=64)
+        agg_scales = keep.tile([P, D_OUT], U8, align_bytes=64)
+        agg_src = agg_raw[:].rearrange("p t (c i) -> p c t i", i=4)
+        agg_dst = agg_grp[:].rearrange("p (c i) t -> p c t i", i=4)
+        split = AGG_VECTOR_COLS // 4
+        nc.vector.tensor_copy(out=agg_dst[:, :split], in_=agg_src[:, :split])
+        nc.scalar.copy(out=agg_dst[:, split:], in_=agg_src[:, split:])
+        nc.vector.quantize_mx(
+            out=agg_codes[:].bitcast(FP8X4),
+            scales=agg_scales[:],
+            in_=agg_grp[:].rearrange("p o t -> p (o t)"),
+        )
+
+        relu_rows = slice(0, QUADRANT)
+        gelu_rows = slice(3 * QUADRANT, 4 * QUADRANT)
+        act = keep.tile([P, PACK, TOKENS], F32)
+        for r in range(PACK):
+            nc.scalar.activation(
+                out=act[:, r, :], in_=h_ps[r][:], func=ACT.Tanh,
+                scale=slope[:, 0:1], bias=tanh_bias[:, r : r + 1],
+            )
+        for r in range(PACK):
+            nc.vector.tensor_scalar(
+                out=act[relu_rows, r, :], in0=h_ps[r][relu_rows, :],
+                scalar1=bias[relu_rows, r : r + 1], scalar2=0.0, op0=ALU.add, op1=ALU.max,
+            )
+        for r in range(PACK):
+            nc.scalar.activation(
+                out=act[gelu_rows, r, :], in_=h_ps[r][gelu_rows, :], func=ACT.Gelu,
+                bias=bias[gelu_rows, r : r + 1],
+            )
+
+        c_grp = keep.tile([P, TOKEN_TILES, P, PACK], BF16, align_bytes=64)
+        c_codes = keep.tile([P, TOKEN_TILES, P], U32, align_bytes=64)
+        c_scales = keep.tile([P, TOKEN_TILES, P], U8, align_bytes=64)
+        for i in range(TOKEN_TILES):
+            nc.vector.tensor_scalar(
+                out=c_grp[:, i, :, :],
+                in0=act[:, :, i * P : (i + 1) * P].rearrange("p r n -> p n r"),
+                scalar1=slope[:, 0:1], scalar2=offset[:, 0:1], op0=ALU.mult, op1=ALU.add,
+            )
+        for i in range(TOKEN_TILES):
+            nc.vector.quantize_mx(
+                out=c_codes[:, i, :].bitcast(FP8X4),
+                scales=c_scales[:, i, :],
+                in_=c_grp[:, i, :, :].rearrange("p n r -> p (n r)"),
+            )
+        for i in range(TOKEN_TILES):
+            out_ps = psum.tile([P, D_OUT], F32, name="out_ps%d" % i)
+            nc.tensor.matmul_mx(
+                out=out_ps[:],
+                lhsT=c_codes[:, i, :].bitcast(FP8X4),
+                lhsT_scale=c_scales[:, i, :],
+                rhs=agg_codes[:].bitcast(FP8X4),
+                rhs_scale=agg_scales[:],
+                start=True,
+                stop=True,
+            )
+            out_sb = keep.tile([P, D_OUT], F32, name="out_sb%d" % i)
+            if i == 0:
+                nc.scalar.copy(out=out_sb[:], in_=out_ps[:])
+            else:
+                nc.vector.tensor_copy(out=out_sb[:], in_=out_ps[:])
+            nc.sync.dma_start(out=out[i * P : (i + 1) * P, :], in_=out_sb[:])

@@ -20,16 +20,16 @@ D_OUT = 512
 TOKEN_TILES = TOKENS // P
 D_PASSES = D_IN // K_PASS
 QUADRANT = 32
+HALF_OUT = D_OUT // 2
 
 FLOPS = 2 * TOKENS * D_IN * BRANCHES + 2 * TOKENS * BRANCHES * D_OUT
 
-W_VECTOR_M = 96
-AGG_VECTOR_COLS = 256
+AGG_SCALAR_COLS = 128
 
 
 def tile_kan_s_kernel(tc, x, W, b, agg, out):
     nc = tc.nc
-    with tc.tile_pool(name="keep", bufs=1) as keep, tc.psum_pool(name="psum", bufs=1) as psum:
+    with tc.tile_pool(name="keep", bufs=1) as keep, tc.psum_pool(name="psum", bufs=1) as psum, tc.manual_schedule():
         ident = keep.tile([P, P], F32)
         make_identity(nc, ident[:])
         slope = keep.tile([P, 1], F32)
@@ -41,6 +41,8 @@ def tile_kan_s_kernel(tc, x, W, b, agg, out):
         warm = keep.tile([P, 1], F32)
         nc.scalar.activation(out=warm[:], in_=offset[:], func=ACT.Gelu)
 
+        b_sb = keep.tile([P, PACK], BF16)
+        nc.sync.dma_start(out=b_sb[:], in_=b.rearrange("(p r) -> p r", r=PACK))
         x_sb = []
         for i in range(TOKEN_TILES):
             x_tile = keep.tile([P, D_IN], BF16, name="x_sb%d" % i)
@@ -54,8 +56,6 @@ def tile_kan_s_kernel(tc, x, W, b, agg, out):
             )
         agg_raw = keep.tile([P, PACK, D_OUT], BF16)
         nc.sync.dma_start(out=agg_raw[:], in_=agg.rearrange("(p t) o -> p t o", t=PACK))
-        b_sb = keep.tile([P, PACK], BF16)
-        nc.scalar.dma_start(out=b_sb[:], in_=b.rearrange("(p r) -> p r", r=PACK))
 
         bias = keep.tile([P, PACK], F32)
         nc.vector.tensor_copy(out=bias[:], in_=b_sb[:])
@@ -64,11 +64,21 @@ def tile_kan_s_kernel(tc, x, W, b, agg, out):
             out=tanh_bias[:], in0=b_sb[:], scalar1=slope[:, 0:1], scalar2=None, op0=ALU.mult
         )
 
-        x_grp = keep.tile([P, D_PASSES * TOKENS * PACK], BF16, align_bytes=64)
-        x_grp_words = x_grp[:].bitcast(F32).rearrange("p (g n u) -> p g n u", g=D_PASSES, u=2)
-        for i in range(TOKEN_TILES):
+        x_grp = keep.tile([P, D_PASSES, TOKENS, PACK], BF16, align_bytes=64)
+        x_grp_words = (
+            x_grp[:].rearrange("p g n t -> p (g n t)").bitcast(F32)
+            .rearrange("p (g n u) -> p g n u", g=D_PASSES, u=2)
+        )
+        x_codes = keep.tile([P, D_PASSES, TOKENS], U32, align_bytes=64)
+        x_scales = keep.tile([P, D_PASSES, TOKENS], U8, align_bytes=64)
+        w_grp = keep.tile([P, D_PASSES, PACK, P, PACK], BF16, align_bytes=64)
+        w_codes = keep.tile([P, D_PASSES, PACK, P], U32, align_bytes=64)
+        w_scales = keep.tile([P, D_PASSES, PACK, P], U8, align_bytes=64)
+        h_ps = [psum.tile([P, TOKENS], F32, name="h_ps%d" % r) for r in range(PACK)]
+
+        def transpose_x(i):
             x_words = x_sb[i][:].bitcast(F32)
-            xt = psum.tile([P, D_PASSES, 2, P], F32, name="xt%d" % i)
+            xt = psum.tile([P, D_PASSES, 2, P], F32, name="xt%d" % i, tag="early%d" % i)
             for g in range(D_PASSES):
                 for u in range(2):
                     first = (2 * g + u) * P
@@ -77,56 +87,56 @@ def tile_kan_s_kernel(tc, x, W, b, agg, out):
                 out=x_grp_words[:, :, i * P : (i + 1) * P, :],
                 in_=xt[:].rearrange("p g u n -> p g n u"),
             )
-        x_codes = keep.tile([P, D_PASSES, TOKENS], U32, align_bytes=64)
-        x_scales = keep.tile([P, D_PASSES, TOKENS], U8, align_bytes=64)
 
-        w_grp = keep.tile([P, D_PASSES, PACK, P, PACK], BF16, align_bytes=64)
-        w_codes = keep.tile([P, D_PASSES, BRANCHES], U32, align_bytes=64)
-        w_scales = keep.tile([P, D_PASSES, BRANCHES], U8, align_bytes=64)
+        def quantise_x(i):
+            tokens = slice(i * P, (i + 1) * P)
+            for g in range(D_PASSES):
+                nc.vector.quantize_mx(
+                    out=x_codes[:, g, tokens].bitcast(FP8X4),
+                    scales=x_scales[:, g, tokens],
+                    in_=x_grp[:, g, tokens, :].rearrange("p n t -> p (n t)"),
+                )
 
-        def regroup_w(g):
-            src = w_raw[:, g, :, :].rearrange("p t (m r) -> p m t r", r=PACK)
-            dst = w_grp[:, g, :, :, :].rearrange("p r m t -> p m t r")
-            nc.vector.tensor_copy(out=dst[:, :W_VECTOR_M], in_=src[:, :W_VECTOR_M])
-            nc.scalar.copy(out=dst[:, W_VECTOR_M:], in_=src[:, W_VECTOR_M:])
-
-        def quantise_w(g):
-            nc.vector.quantize_mx(
-                out=w_codes[:, g, :].bitcast(FP8X4),
-                scales=w_scales[:, g, :],
-                in_=w_grp[:, g, :, :, :].rearrange("p r m t -> p (r m t)"),
+        def regroup_w(copy, g, pair):
+            rs = slice(2 * pair, 2 * pair + 2)
+            copy(
+                out=w_grp[:, g, rs, :, :].rearrange("p r m t -> p m t r"),
+                in_=w_raw[:, g, :, :].rearrange("p t (m r) -> p m t r", r=PACK)[:, :, :, rs],
             )
 
-        def quantise_x(g):
-            width = TOKENS * PACK
+        def quantise_w(g, pair):
+            rs = slice(2 * pair, 2 * pair + 2)
             nc.vector.quantize_mx(
-                out=x_codes[:, g, :].bitcast(FP8X4),
-                scales=x_scales[:, g, :],
-                in_=x_grp[:, g * width : (g + 1) * width],
+                out=w_codes[:, g, rs, :].rearrange("p r m -> p (r m)").bitcast(FP8X4),
+                scales=w_scales[:, g, rs, :].rearrange("p r m -> p (r m)"),
+                in_=w_grp[:, g, rs, :, :].rearrange("p r m t -> p (r m t)"),
             )
-
-        h_ps = [psum.tile([P, TOKENS], F32, name="h_ps%d" % r) for r in range(PACK)]
 
         def first_product(g):
             for r in range(PACK):
-                cols = slice(r * P, (r + 1) * P)
                 nc.tensor.matmul_mx(
                     out=h_ps[r][:],
-                    lhsT=w_codes[:, g, cols].bitcast(FP8X4),
-                    lhsT_scale=w_scales[:, g, cols],
+                    lhsT=w_codes[:, g, r, :].bitcast(FP8X4),
+                    lhsT_scale=w_scales[:, g, r, :],
                     rhs=x_codes[:, g, :].bitcast(FP8X4),
                     rhs_scale=x_scales[:, g, :],
                     start=(g == 0),
                     stop=(g == D_PASSES - 1),
                 )
 
-        regroup_w(0)
+        transpose_x(0)
+        transpose_x(1)
         quantise_x(0)
+        regroup_w(nc.vector.tensor_copy, 0, 0)
+        regroup_w(nc.scalar.copy, 0, 1)
         quantise_x(1)
-        quantise_w(0)
+        quantise_w(0, 0)
+        regroup_w(nc.vector.tensor_copy, 1, 0)
+        regroup_w(nc.scalar.copy, 1, 1)
+        quantise_w(0, 1)
         first_product(0)
-        regroup_w(1)
-        quantise_w(1)
+        quantise_w(1, 0)
+        quantise_w(1, 1)
         first_product(1)
 
         agg_grp = keep.tile([P, D_OUT, PACK], BF16, align_bytes=64)
@@ -134,14 +144,9 @@ def tile_kan_s_kernel(tc, x, W, b, agg, out):
         agg_scales = keep.tile([P, D_OUT], U8, align_bytes=64)
         agg_src = agg_raw[:].rearrange("p t (c i) -> p c t i", i=4)
         agg_dst = agg_grp[:].rearrange("p (c i) t -> p c t i", i=4)
-        split = AGG_VECTOR_COLS // 4
-        nc.vector.tensor_copy(out=agg_dst[:, :split], in_=agg_src[:, :split])
-        nc.scalar.copy(out=agg_dst[:, split:], in_=agg_src[:, split:])
-        nc.vector.quantize_mx(
-            out=agg_codes[:].bitcast(FP8X4),
-            scales=agg_scales[:],
-            in_=agg_grp[:].rearrange("p o t -> p (o t)"),
-        )
+        split = AGG_SCALAR_COLS // 4
+        nc.scalar.copy(out=agg_dst[:, :split], in_=agg_src[:, :split])
+        nc.vector.tensor_copy(out=agg_dst[:, split:], in_=agg_src[:, split:])
 
         relu_rows = slice(0, QUADRANT)
         gelu_rows = slice(3 * QUADRANT, 4 * QUADRANT)
@@ -151,46 +156,53 @@ def tile_kan_s_kernel(tc, x, W, b, agg, out):
                 out=act[:, r, :], in_=h_ps[r][:], func=ACT.Tanh,
                 scale=slope[:, 0:1], bias=tanh_bias[:, r : r + 1],
             )
-        for r in range(PACK):
             nc.vector.tensor_scalar(
                 out=act[relu_rows, r, :], in0=h_ps[r][relu_rows, :],
                 scalar1=bias[relu_rows, r : r + 1], scalar2=0.0, op0=ALU.add, op1=ALU.max,
             )
-        for r in range(PACK):
-            nc.scalar.activation(
-                out=act[gelu_rows, r, :], in_=h_ps[r][gelu_rows, :], func=ACT.Gelu,
-                bias=bias[gelu_rows, r : r + 1],
-            )
+        nc.vector.quantize_mx(
+            out=agg_codes[:].bitcast(FP8X4),
+            scales=agg_scales[:],
+            in_=agg_grp[:].rearrange("p o t -> p (o t)"),
+        )
 
         c_grp = keep.tile([P, TOKEN_TILES, P, PACK], BF16, align_bytes=64)
         c_codes = keep.tile([P, TOKEN_TILES, P], U32, align_bytes=64)
         c_scales = keep.tile([P, TOKEN_TILES, P], U8, align_bytes=64)
         for i in range(TOKEN_TILES):
+            tokens = slice(i * P, (i + 1) * P)
+            for r in range(PACK):
+                nc.scalar.activation(
+                    out=act[gelu_rows, r, tokens], in_=h_ps[r][gelu_rows, tokens], func=ACT.Gelu,
+                    bias=bias[gelu_rows, r : r + 1],
+                )
             nc.vector.tensor_scalar(
                 out=c_grp[:, i, :, :],
-                in0=act[:, :, i * P : (i + 1) * P].rearrange("p r n -> p n r"),
+                in0=act[:, :, tokens].rearrange("p r n -> p n r"),
                 scalar1=slope[:, 0:1], scalar2=offset[:, 0:1], op0=ALU.mult, op1=ALU.add,
             )
-        for i in range(TOKEN_TILES):
             nc.vector.quantize_mx(
                 out=c_codes[:, i, :].bitcast(FP8X4),
                 scales=c_scales[:, i, :],
                 in_=c_grp[:, i, :, :].rearrange("p n r -> p (n r)"),
             )
         for i in range(TOKEN_TILES):
-            out_ps = psum.tile([P, D_OUT], F32, name="out_ps%d" % i)
-            nc.tensor.matmul_mx(
-                out=out_ps[:],
-                lhsT=c_codes[:, i, :].bitcast(FP8X4),
-                lhsT_scale=c_scales[:, i, :],
-                rhs=agg_codes[:].bitcast(FP8X4),
-                rhs_scale=agg_scales[:],
-                start=True,
-                stop=True,
-            )
             out_sb = keep.tile([P, D_OUT], F32, name="out_sb%d" % i)
-            if i == 0:
-                nc.scalar.copy(out=out_sb[:], in_=out_ps[:])
-            else:
-                nc.vector.tensor_copy(out=out_sb[:], in_=out_ps[:])
+            for j in range(2):
+                cols = slice(j * HALF_OUT, (j + 1) * HALF_OUT)
+                tag = ("early%d" if i == 0 else "late%d") % j
+                out_ps = psum.tile([P, HALF_OUT], F32, name="out_ps%d%d" % (i, j), tag=tag)
+                nc.tensor.matmul_mx(
+                    out=out_ps[:],
+                    lhsT=c_codes[:, i, :].bitcast(FP8X4),
+                    lhsT_scale=c_scales[:, i, :],
+                    rhs=agg_codes[:, cols].bitcast(FP8X4),
+                    rhs_scale=agg_scales[:, cols],
+                    start=True,
+                    stop=True,
+                )
+                if i == 1 and j == 1:
+                    nc.vector.tensor_copy(out=out_sb[:, cols], in_=out_ps[:])
+                else:
+                    nc.scalar.copy(out=out_sb[:, cols], in_=out_ps[:])
             nc.sync.dma_start(out=out[i * P : (i + 1) * P, :], in_=out_sb[:])

@@ -19,7 +19,6 @@ BRANCHES = 512
 D_OUT = 512
 TOKEN_TILES = TOKENS // P
 D_PASSES = D_IN // K_PASS
-QUADRANT = 32
 HALF_OUT = D_OUT // 2
 
 FLOPS = 2 * TOKENS * D_IN * BRANCHES + 2 * TOKENS * BRANCHES * D_OUT
@@ -32,22 +31,21 @@ def tile_kan_s_kernel(tc, x, W, b, agg, out):
     with tc.tile_pool(name="keep", bufs=1) as keep, tc.psum_pool(name="psum", bufs=1) as psum, tc.manual_schedule():
         ident = keep.tile([P, P], F32)
         make_identity(nc, ident[:])
-        slope = keep.tile([P, 1], F32)
-        offset = keep.tile([P, 1], F32)
-        nc.vector.memset(slope[:], 1.0)
-        nc.vector.memset(slope[2 * QUADRANT : 3 * QUADRANT, :], 0.5)
-        nc.vector.memset(offset[:], 0.0)
-        nc.vector.memset(offset[2 * QUADRANT : 3 * QUADRANT, :], 0.5)
+        zero = keep.tile([P, 1], F32)
+        nc.vector.memset(zero[:], 0.0)
         warm = keep.tile([P, 1], F32)
-        nc.scalar.activation(out=warm[:], in_=offset[:], func=ACT.Gelu)
+        nc.scalar.activation(out=warm[:], in_=zero[:], func=ACT.Gelu)
+        b_rows = keep.tile([P, P], BF16)
+        nc.vector.memset(b_rows[:], 0.0)
+        pick = keep.tile([P, PACK], BF16)
+        nc.vector.tensor_copy(out=pick[:], in_=ident[:, 0:PACK])
 
-        b_sb = keep.tile([P, PACK], BF16)
-        nc.sync.dma_start(out=b_sb[:], in_=b.rearrange("(p r) -> p r", r=PACK))
         x_sb = []
         for i in range(TOKEN_TILES):
             x_tile = keep.tile([P, D_IN], BF16, name="x_sb%d" % i)
             nc.sync.dma_start(out=x_tile[:], in_=x[i * P : (i + 1) * P, :])
             x_sb.append(x_tile)
+        nc.sync.dma_start(out=b_rows[0:PACK, :], in_=b.rearrange("(f p) -> f p", f=PACK))
         w_raw = keep.tile([P, D_PASSES, PACK, BRANCHES], BF16)
         for g in range(D_PASSES):
             nc.sync.dma_start(
@@ -55,14 +53,7 @@ def tile_kan_s_kernel(tc, x, W, b, agg, out):
                 in_=W[g * K_PASS : (g + 1) * K_PASS, :].rearrange("(u p e) c -> p u (e c)", u=2, e=2),
             )
         agg_raw = keep.tile([P, PACK, D_OUT], BF16)
-        nc.sync.dma_start(out=agg_raw[:], in_=agg.rearrange("(p t) o -> p t o", t=PACK))
-
-        bias = keep.tile([P, PACK], F32)
-        nc.vector.tensor_copy(out=bias[:], in_=b_sb[:])
-        tanh_bias = keep.tile([P, PACK], F32)
-        nc.vector.tensor_scalar(
-            out=tanh_bias[:], in0=b_sb[:], scalar1=slope[:, 0:1], scalar2=None, op0=ALU.mult
-        )
+        nc.sync.dma_start(out=agg_raw[:], in_=agg.rearrange("(t p) o -> p t o", t=PACK))
 
         x_grp = keep.tile([P, D_PASSES, TOKENS, PACK], BF16, align_bytes=64)
         x_grp_words = (
@@ -71,9 +62,9 @@ def tile_kan_s_kernel(tc, x, W, b, agg, out):
         )
         x_codes = keep.tile([P, D_PASSES, TOKENS], U32, align_bytes=64)
         x_scales = keep.tile([P, D_PASSES, TOKENS], U8, align_bytes=64)
-        w_grp = keep.tile([P, D_PASSES, PACK, P, PACK], BF16, align_bytes=64)
-        w_codes = keep.tile([P, D_PASSES, PACK, P], U32, align_bytes=64)
-        w_scales = keep.tile([P, D_PASSES, PACK, P], U8, align_bytes=64)
+        w_grp = keep.tile([P, D_PASSES, BRANCHES, PACK], BF16, align_bytes=64)
+        w_codes = keep.tile([P, D_PASSES, BRANCHES], U32, align_bytes=64)
+        w_scales = keep.tile([P, D_PASSES, BRANCHES], U8, align_bytes=64)
         h_ps = [psum.tile([P, TOKENS], F32, name="h_ps%d" % r) for r in range(PACK)]
 
         def transpose_x(i):
@@ -98,26 +89,26 @@ def tile_kan_s_kernel(tc, x, W, b, agg, out):
                 )
 
         def regroup_w(copy, g, pair):
-            rs = slice(2 * pair, 2 * pair + 2)
+            half = slice(2 * pair * P, (2 * pair + 2) * P)
             copy(
-                out=w_grp[:, g, rs, :, :].rearrange("p r m t -> p m t r"),
-                in_=w_raw[:, g, :, :].rearrange("p t (m r) -> p m t r", r=PACK)[:, :, :, rs],
+                out=w_grp[:, g, half, :].rearrange("p (c i) t -> p c t i", i=4),
+                in_=w_raw[:, g, :, half].rearrange("p t (c i) -> p c t i", i=4),
             )
 
         def quantise_w(g, pair):
-            rs = slice(2 * pair, 2 * pair + 2)
+            half = slice(2 * pair * P, (2 * pair + 2) * P)
             nc.vector.quantize_mx(
-                out=w_codes[:, g, rs, :].rearrange("p r m -> p (r m)").bitcast(FP8X4),
-                scales=w_scales[:, g, rs, :].rearrange("p r m -> p (r m)"),
-                in_=w_grp[:, g, rs, :, :].rearrange("p r m t -> p (r m t)"),
+                out=w_codes[:, g, half].bitcast(FP8X4),
+                scales=w_scales[:, g, half],
+                in_=w_grp[:, g, half, :].rearrange("p c t -> p (c t)"),
             )
 
         def first_product(g):
             for r in range(PACK):
                 nc.tensor.matmul_mx(
                     out=h_ps[r][:],
-                    lhsT=w_codes[:, g, r, :].bitcast(FP8X4),
-                    lhsT_scale=w_scales[:, g, r, :],
+                    lhsT=w_codes[:, g, r * P : (r + 1) * P].bitcast(FP8X4),
+                    lhsT_scale=w_scales[:, g, r * P : (r + 1) * P],
                     rhs=x_codes[:, g, :].bitcast(FP8X4),
                     rhs_scale=x_scales[:, g, :],
                     start=(g == 0),
@@ -126,10 +117,18 @@ def tile_kan_s_kernel(tc, x, W, b, agg, out):
 
         transpose_x(0)
         transpose_x(1)
+        bias_ps = psum.tile([P, PACK], F32, name="bias_ps", tag="late0")
+        nc.tensor.matmul(bias_ps[:], lhsT=b_rows[:], rhs=pick[:], start=True, stop=True)
         quantise_x(0)
         regroup_w(nc.vector.tensor_copy, 0, 0)
         regroup_w(nc.scalar.copy, 0, 1)
         quantise_x(1)
+        bias = keep.tile([P, PACK], F32)
+        nc.vector.tensor_copy(out=bias[:], in_=bias_ps[:])
+        half_bias = keep.tile([P, 1], F32)
+        nc.vector.tensor_scalar(
+            out=half_bias[:], in0=bias_ps[:, 2:3], scalar1=0.5, scalar2=None, op0=ALU.mult
+        )
         quantise_w(0, 0)
         regroup_w(nc.vector.tensor_copy, 1, 0)
         regroup_w(nc.scalar.copy, 1, 1)
@@ -148,44 +147,57 @@ def tile_kan_s_kernel(tc, x, W, b, agg, out):
         nc.scalar.copy(out=agg_dst[:, :split], in_=agg_src[:, :split])
         nc.vector.tensor_copy(out=agg_dst[:, split:], in_=agg_src[:, split:])
 
-        relu_rows = slice(0, QUADRANT)
-        gelu_rows = slice(3 * QUADRANT, 4 * QUADRANT)
-        act = keep.tile([P, PACK, TOKENS], F32)
-        for r in range(PACK):
+        act = keep.tile([P, PACK, TOKENS], BF16)
+        sig = keep.tile([P, TOKENS], F32)
+        c_grp = keep.tile([P, TOKEN_TILES, P, PACK], BF16, align_bytes=64)
+        c_codes = keep.tile([P, TOKEN_TILES, P], U32, align_bytes=64)
+        c_scales = keep.tile([P, TOKEN_TILES, P], U8, align_bytes=64)
+
+        def scalar_activations(tokens):
             nc.scalar.activation(
-                out=act[:, r, :], in_=h_ps[r][:], func=ACT.Tanh,
-                scale=slope[:, 0:1], bias=tanh_bias[:, r : r + 1],
+                out=sig[:, tokens], in_=h_ps[2][:, tokens], func=ACT.Tanh, scale=0.5, bias=half_bias[:, 0:1]
             )
+            nc.scalar.activation(
+                out=act[:, 1, tokens], in_=h_ps[1][:, tokens], func=ACT.Tanh, bias=bias[:, 1:2]
+            )
+            nc.scalar.activation(
+                out=act[:, 3, tokens], in_=h_ps[3][:, tokens], func=ACT.Gelu, bias=bias[:, 3:4]
+            )
+
+        def sigmoid_end(tokens):
             nc.vector.tensor_scalar(
-                out=act[relu_rows, r, :], in0=h_ps[r][relu_rows, :],
-                scalar1=bias[relu_rows, r : r + 1], scalar2=0.0, op0=ALU.add, op1=ALU.max,
+                out=act[:, 2, tokens], in0=sig[:, tokens], scalar1=0.5, scalar2=0.5, op0=ALU.mult, op1=ALU.add
             )
+
+        def regroup_c(i):
+            nc.vector.tensor_copy(
+                out=c_grp[:, i, :, :], in_=act[:, :, i * P : (i + 1) * P].rearrange("p t n -> p n t")
+            )
+
+        def quantise_c(i):
+            nc.vector.quantize_mx(
+                out=c_codes[:, i, :].bitcast(FP8X4),
+                scales=c_scales[:, i, :],
+                in_=c_grp[:, i, :, :].rearrange("p n t -> p (n t)"),
+            )
+
+        for i in range(TOKEN_TILES):
+            scalar_activations(slice(i * P, (i + 1) * P))
+        nc.vector.tensor_scalar(
+            out=act[:, 0, :], in0=h_ps[0][:], scalar1=bias[:, 0:1], scalar2=0.0, op0=ALU.add, op1=ALU.max
+        )
         nc.vector.quantize_mx(
             out=agg_codes[:].bitcast(FP8X4),
             scales=agg_scales[:],
             in_=agg_grp[:].rearrange("p o t -> p (o t)"),
         )
+        sigmoid_end(slice(0, P))
+        regroup_c(0)
+        sigmoid_end(slice(P, TOKENS))
+        quantise_c(0)
+        regroup_c(1)
+        quantise_c(1)
 
-        c_grp = keep.tile([P, TOKEN_TILES, P, PACK], BF16, align_bytes=64)
-        c_codes = keep.tile([P, TOKEN_TILES, P], U32, align_bytes=64)
-        c_scales = keep.tile([P, TOKEN_TILES, P], U8, align_bytes=64)
-        for i in range(TOKEN_TILES):
-            tokens = slice(i * P, (i + 1) * P)
-            for r in range(PACK):
-                nc.scalar.activation(
-                    out=act[gelu_rows, r, tokens], in_=h_ps[r][gelu_rows, tokens], func=ACT.Gelu,
-                    bias=bias[gelu_rows, r : r + 1],
-                )
-            nc.vector.tensor_scalar(
-                out=c_grp[:, i, :, :],
-                in0=act[:, :, tokens].rearrange("p r n -> p n r"),
-                scalar1=slope[:, 0:1], scalar2=offset[:, 0:1], op0=ALU.mult, op1=ALU.add,
-            )
-            nc.vector.quantize_mx(
-                out=c_codes[:, i, :].bitcast(FP8X4),
-                scales=c_scales[:, i, :],
-                in_=c_grp[:, i, :, :].rearrange("p n r -> p (n r)"),
-            )
         for i in range(TOKEN_TILES):
             out_sb = keep.tile([P, D_OUT], F32, name="out_sb%d" % i)
             for j in range(2):

@@ -23,7 +23,7 @@ HALF_OUT = D_OUT // 2
 
 FLOPS = 2 * TOKENS * D_IN * BRANCHES + 2 * TOKENS * BRANCHES * D_OUT
 
-AGG_SCALAR_COLS = 128
+AGG_SCALAR_COLS = 256
 
 
 def tile_kan_s_kernel(tc, x, W, b, agg, out):
@@ -33,6 +33,8 @@ def tile_kan_s_kernel(tc, x, W, b, agg, out):
         make_identity(nc, ident[:])
         zero = keep.tile([P, 1], F32)
         nc.vector.memset(zero[:], 0.0)
+        half = keep.tile([P, 1], F32)
+        nc.vector.memset(half[:], 0.5)
         warm = keep.tile([P, 1], F32)
         nc.scalar.activation(out=warm[:], in_=zero[:], func=ACT.Gelu)
         b_rows = keep.tile([P, P], BF16)
@@ -65,19 +67,22 @@ def tile_kan_s_kernel(tc, x, W, b, agg, out):
         w_grp = keep.tile([P, D_PASSES, BRANCHES, PACK], BF16, align_bytes=64)
         w_codes = keep.tile([P, D_PASSES, BRANCHES], U32, align_bytes=64)
         w_scales = keep.tile([P, D_PASSES, BRANCHES], U8, align_bytes=64)
-        h_ps = [psum.tile([P, TOKENS], F32, name="h_ps%d" % r) for r in range(PACK)]
+        h_ps = []
+        for f in range(PACK):
+            h_tile = psum.tile([P, TOKENS], F32, name="h_ps%d" % f)
+            h_ps.append(h_tile)
 
         def transpose_x(i):
             x_words = x_sb[i][:].bitcast(F32)
-            xt = psum.tile([P, D_PASSES, 2, P], F32, name="xt%d" % i, tag="early%d" % i)
             for g in range(D_PASSES):
+                xt = psum.tile([P, 2, P], F32, name="xt%d%d" % (i, g), tag="bank%d%d" % (i, g))
                 for u in range(2):
                     first = (2 * g + u) * P
-                    nc.tensor.transpose(xt[:, g, u, :], x_words[:, first : first + P], ident[:])
-            nc.scalar.copy(
-                out=x_grp_words[:, :, i * P : (i + 1) * P, :],
-                in_=xt[:].rearrange("p g u n -> p g n u"),
-            )
+                    nc.tensor.transpose(xt[:, u, :], x_words[:, first : first + P], ident[:])
+                nc.scalar.copy(
+                    out=x_grp_words[:, g, i * P : (i + 1) * P, :],
+                    in_=xt[:].rearrange("p u n -> p n u"),
+                )
 
         def quantise_x(i):
             tokens = slice(i * P, (i + 1) * P)
@@ -89,22 +94,22 @@ def tile_kan_s_kernel(tc, x, W, b, agg, out):
                 )
 
         def regroup_w(copy, g, pair):
-            half = slice(2 * pair * P, (2 * pair + 2) * P)
+            cols = slice(2 * pair * P, (2 * pair + 2) * P)
             copy(
-                out=w_grp[:, g, half, :].rearrange("p (c i) t -> p c t i", i=4),
-                in_=w_raw[:, g, :, half].rearrange("p t (c i) -> p c t i", i=4),
+                out=w_grp[:, g, cols, :].rearrange("p (c i) t -> p c t i", i=4),
+                in_=w_raw[:, g, :, cols].rearrange("p t (c i) -> p c t i", i=4),
             )
 
         def quantise_w(g, pair):
-            half = slice(2 * pair * P, (2 * pair + 2) * P)
+            cols = slice(2 * pair * P, (2 * pair + 2) * P)
             nc.vector.quantize_mx(
-                out=w_codes[:, g, half].bitcast(FP8X4),
-                scales=w_scales[:, g, half],
-                in_=w_grp[:, g, half, :].rearrange("p c t -> p (c t)"),
+                out=w_codes[:, g, cols].bitcast(FP8X4),
+                scales=w_scales[:, g, cols],
+                in_=w_grp[:, g, cols, :].rearrange("p c t -> p (c t)"),
             )
 
-        def first_product(g):
-            for r in range(PACK):
+        def first_product(g, functions):
+            for r in functions:
                 nc.tensor.matmul_mx(
                     out=h_ps[r][:],
                     lhsT=w_codes[:, g, r * P : (r + 1) * P].bitcast(FP8X4),
@@ -117,26 +122,26 @@ def tile_kan_s_kernel(tc, x, W, b, agg, out):
 
         transpose_x(0)
         transpose_x(1)
-        bias_ps = psum.tile([P, PACK], F32, name="bias_ps", tag="late0")
+        bias_ps = psum.tile([P, PACK], F32, name="bias_ps", tag="bank00")
         nc.tensor.matmul(bias_ps[:], lhsT=b_rows[:], rhs=pick[:], start=True, stop=True)
         quantise_x(0)
         regroup_w(nc.vector.tensor_copy, 0, 0)
         regroup_w(nc.scalar.copy, 0, 1)
         quantise_x(1)
-        bias = keep.tile([P, PACK], F32)
-        nc.vector.tensor_copy(out=bias[:], in_=bias_ps[:])
-        half_bias = keep.tile([P, 1], F32)
-        nc.vector.tensor_scalar(
-            out=half_bias[:], in0=bias_ps[:, 2:3], scalar1=0.5, scalar2=None, op0=ALU.mult
-        )
         quantise_w(0, 0)
+        first_product(0, (0, 1))
+        quantise_w(0, 1)
+        first_product(0, (2, 3))
         regroup_w(nc.vector.tensor_copy, 1, 0)
         regroup_w(nc.scalar.copy, 1, 1)
-        quantise_w(0, 1)
-        first_product(0)
-        quantise_w(1, 0)
         quantise_w(1, 1)
-        first_product(1)
+        first_product(1, (2, 3))
+        quantise_w(1, 0)
+        first_product(1, (0, 1))
+        bias = keep.tile([P, PACK], F32)
+        half_bias = keep.tile([P, 1], F32)
+        nc.scalar.copy(out=bias[:], in_=bias_ps[:])
+        nc.scalar.mul(out=half_bias[:], in_=bias[:, 2:3], mul=0.5)
 
         agg_grp = keep.tile([P, D_OUT, PACK], BF16, align_bytes=64)
         agg_codes = keep.tile([P, D_OUT], U32, align_bytes=64)
@@ -158,19 +163,17 @@ def tile_kan_s_kernel(tc, x, W, b, agg, out):
                 out=sig[:, tokens], in_=h_ps[2][:, tokens], func=ACT.Tanh, scale=0.5, bias=half_bias[:, 0:1]
             )
             nc.scalar.activation(
+                out=act[:, 3, tokens], in_=h_ps[3][:, tokens], func=ACT.Gelu, bias=bias[:, 3:4]
+            )
+            nc.scalar.activation(
                 out=act[:, 1, tokens], in_=h_ps[1][:, tokens], func=ACT.Tanh, bias=bias[:, 1:2]
             )
             nc.scalar.activation(
-                out=act[:, 3, tokens], in_=h_ps[3][:, tokens], func=ACT.Gelu, bias=bias[:, 3:4]
+                out=act[:, 2, tokens], in_=sig[:, tokens], func=ACT.Identity, scale=0.5, bias=half[:, 0:1]
             )
 
-        def sigmoid_end(tokens):
-            nc.vector.tensor_scalar(
-                out=act[:, 2, tokens], in0=sig[:, tokens], scalar1=0.5, scalar2=0.5, op0=ALU.mult, op1=ALU.add
-            )
-
-        def regroup_c(i):
-            nc.vector.tensor_copy(
+        def regroup_c(copy, i):
+            copy(
                 out=c_grp[:, i, :, :], in_=act[:, :, i * P : (i + 1) * P].rearrange("p t n -> p n t")
             )
 
@@ -191,19 +194,16 @@ def tile_kan_s_kernel(tc, x, W, b, agg, out):
             scales=agg_scales[:],
             in_=agg_grp[:].rearrange("p o t -> p (o t)"),
         )
-        sigmoid_end(slice(0, P))
-        regroup_c(0)
-        sigmoid_end(slice(P, TOKENS))
+        regroup_c(nc.vector.tensor_copy, 0)
+        regroup_c(nc.scalar.copy, 1)
         quantise_c(0)
-        regroup_c(1)
         quantise_c(1)
 
         for i in range(TOKEN_TILES):
             out_sb = keep.tile([P, D_OUT], F32, name="out_sb%d" % i)
             for j in range(2):
                 cols = slice(j * HALF_OUT, (j + 1) * HALF_OUT)
-                tag = ("early%d" if i == 0 else "late%d") % j
-                out_ps = psum.tile([P, HALF_OUT], F32, name="out_ps%d%d" % (i, j), tag=tag)
+                out_ps = psum.tile([P, HALF_OUT], F32, name="out_ps%d%d" % (i, j), tag="bank%d%d" % (i, j))
                 nc.tensor.matmul_mx(
                     out=out_ps[:],
                     lhsT=c_codes[:, i, :].bitcast(FP8X4),
@@ -213,7 +213,7 @@ def tile_kan_s_kernel(tc, x, W, b, agg, out):
                     start=True,
                     stop=True,
                 )
-                if i == 1 and j == 1:
+                if j == 1:
                     nc.vector.tensor_copy(out=out_sb[:, cols], in_=out_ps[:])
                 else:
                     nc.scalar.copy(out=out_sb[:, cols], in_=out_ps[:])

@@ -19,11 +19,13 @@ BRANCHES = 512
 D_OUT = 512
 TOKEN_TILES = TOKENS // P
 D_PASSES = D_IN // K_PASS
+RELU, TANH, SIGMOID, GELU = range(4)
 HALF_OUT = D_OUT // 2
+BANK = 512
 
 FLOPS = 2 * TOKENS * D_IN * BRANCHES + 2 * TOKENS * BRANCHES * D_OUT
 
-AGG_SCALAR_COLS = 256
+AGG_SCALAR_COLS = 128
 
 
 def tile_kan_s_kernel(tc, x, W, b, agg, out):
@@ -45,15 +47,23 @@ def tile_kan_s_kernel(tc, x, W, b, agg, out):
         x_sb = []
         for i in range(TOKEN_TILES):
             x_tile = keep.tile([P, D_IN], BF16, name="x_sb%d" % i)
-            nc.sync.dma_start(out=x_tile[:], in_=x[i * P : (i + 1) * P, :])
             x_sb.append(x_tile)
-        nc.sync.dma_start(out=b_rows[0:PACK, :], in_=b.rearrange("(f p) -> f p", f=PACK))
         w_raw = keep.tile([P, D_PASSES, PACK, BRANCHES], BF16)
-        for g in range(D_PASSES):
+
+        def load_w(g, f):
+            cols = slice(f * P, (f + 2) * P)
             nc.sync.dma_start(
-                out=w_raw[:, g, :, :].rearrange("p (u e) c -> p u (e c)", e=2),
-                in_=W[g * K_PASS : (g + 1) * K_PASS, :].rearrange("(u p e) c -> p u (e c)", u=2, e=2),
+                out=w_raw[:, g, :, cols],
+                in_=W[g * K_PASS : (g + 1) * K_PASS, cols].rearrange("(p t) c -> p t c", t=PACK),
             )
+
+        load_w(0, SIGMOID)
+        nc.sync.dma_start(out=b_rows[0:PACK, :], in_=b.rearrange("(f p) -> f p", f=PACK))
+        for i in range(TOKEN_TILES):
+            nc.sync.dma_start(out=x_sb[i][:], in_=x[i * P : (i + 1) * P, :])
+        load_w(0, RELU)
+        load_w(1, SIGMOID)
+        load_w(1, RELU)
         agg_raw = keep.tile([P, PACK, D_OUT], BF16)
         nc.sync.dma_start(out=agg_raw[:], in_=agg.rearrange("(t p) o -> p t o", t=PACK))
 
@@ -67,21 +77,21 @@ def tile_kan_s_kernel(tc, x, W, b, agg, out):
         w_grp = keep.tile([P, D_PASSES, BRANCHES, PACK], BF16, align_bytes=64)
         w_codes = keep.tile([P, D_PASSES, BRANCHES], U32, align_bytes=64)
         w_scales = keep.tile([P, D_PASSES, BRANCHES], U8, align_bytes=64)
-        h_ps = []
-        for f in range(PACK):
-            h_tile = psum.tile([P, TOKENS], F32, name="h_ps%d" % f)
-            h_ps.append(h_tile)
+
+        def bank(number, label):
+            tile = psum.tile([P, BANK], F32, name=label, tag="bank%d" % number)
+            return tile
 
         def transpose_x(i):
             x_words = x_sb[i][:].bitcast(F32)
             for g in range(D_PASSES):
-                xt = psum.tile([P, 2, P], F32, name="xt%d%d" % (i, g), tag="bank%d%d" % (i, g))
+                xt = bank(2 * i + g, "xt%d%d" % (i, g))[:, 0 : 2 * P].rearrange("p (u n) -> p u n", u=2)
                 for u in range(2):
-                    first = (2 * g + u) * P
-                    nc.tensor.transpose(xt[:, u, :], x_words[:, first : first + P], ident[:])
+                    first = 2 * P * g + u
+                    nc.tensor.transpose(xt[:, u, :], x_words[:, first : 2 * P * (g + 1) : 2], ident[:])
                 nc.scalar.copy(
                     out=x_grp_words[:, g, i * P : (i + 1) * P, :],
-                    in_=xt[:].rearrange("p u n -> p n u"),
+                    in_=xt.rearrange("p u n -> p n u"),
                 )
 
         def quantise_x(i):
@@ -93,55 +103,73 @@ def tile_kan_s_kernel(tc, x, W, b, agg, out):
                     in_=x_grp[:, g, tokens, :].rearrange("p n t -> p (n t)"),
                 )
 
-        def regroup_w(copy, g, pair):
-            cols = slice(2 * pair * P, (2 * pair + 2) * P)
+        def regroup_w(copy, g, f):
+            cols = slice(f * P, (f + 1) * P)
             copy(
                 out=w_grp[:, g, cols, :].rearrange("p (c i) t -> p c t i", i=4),
                 in_=w_raw[:, g, :, cols].rearrange("p t (c i) -> p c t i", i=4),
             )
 
-        def quantise_w(g, pair):
-            cols = slice(2 * pair * P, (2 * pair + 2) * P)
+        def quantise_w(g, f):
+            cols = slice(f * P, (f + 1) * P)
             nc.vector.quantize_mx(
                 out=w_codes[:, g, cols].bitcast(FP8X4),
                 scales=w_scales[:, g, cols],
                 in_=w_grp[:, g, cols, :].rearrange("p c t -> p (c t)"),
             )
 
-        def first_product(g, functions):
-            for r in functions:
-                nc.tensor.matmul_mx(
-                    out=h_ps[r][:],
-                    lhsT=w_codes[:, g, r * P : (r + 1) * P].bitcast(FP8X4),
-                    lhsT_scale=w_scales[:, g, r * P : (r + 1) * P],
-                    rhs=x_codes[:, g, :].bitcast(FP8X4),
-                    rhs_scale=x_scales[:, g, :],
-                    start=(g == 0),
-                    stop=(g == D_PASSES - 1),
-                )
+        h_ps = {}
 
-        transpose_x(0)
-        transpose_x(1)
-        bias_ps = psum.tile([P, PACK], F32, name="bias_ps", tag="bank00")
-        nc.tensor.matmul(bias_ps[:], lhsT=b_rows[:], rhs=pick[:], start=True, stop=True)
-        quantise_x(0)
-        regroup_w(nc.vector.tensor_copy, 0, 0)
-        regroup_w(nc.scalar.copy, 0, 1)
-        quantise_x(1)
-        quantise_w(0, 0)
-        first_product(0, (0, 1))
-        quantise_w(0, 1)
-        first_product(0, (2, 3))
-        regroup_w(nc.vector.tensor_copy, 1, 0)
-        regroup_w(nc.scalar.copy, 1, 1)
-        quantise_w(1, 1)
-        first_product(1, (2, 3))
-        quantise_w(1, 0)
-        first_product(1, (0, 1))
+        def first_product(g, f, i):
+            cols = slice(f * P, (f + 1) * P)
+            tokens = slice(i * P, (i + 1) * P)
+            nc.tensor.matmul_mx(
+                out=h_ps[f, i],
+                lhsT=w_codes[:, g, cols].bitcast(FP8X4),
+                lhsT_scale=w_scales[:, g, cols],
+                rhs=x_codes[:, g, tokens].bitcast(FP8X4),
+                rhs_scale=x_scales[:, g, tokens],
+                start=(g == 0),
+                stop=(g == D_PASSES - 1),
+            )
+
+        bias_ps = bank(7, "bias_ps")[:, 0:PACK]
+        nc.tensor.matmul(bias_ps, lhsT=b_rows[:], rhs=pick[:], start=True, stop=True)
         bias = keep.tile([P, PACK], F32)
         half_bias = keep.tile([P, 1], F32)
-        nc.scalar.copy(out=bias[:], in_=bias_ps[:])
-        nc.scalar.mul(out=half_bias[:], in_=bias[:, 2:3], mul=0.5)
+
+        regroup_w(nc.vector.tensor_copy, 0, SIGMOID)
+        regroup_w(nc.scalar.copy, 0, GELU)
+        nc.scalar.copy(out=bias[:], in_=bias_ps)
+        nc.scalar.mul(out=half_bias[:], in_=bias[:, SIGMOID : SIGMOID + 1], mul=0.5)
+        quantise_w(0, SIGMOID)
+        quantise_w(0, GELU)
+        transpose_x(0)
+        transpose_x(1)
+        for i in range(TOKEN_TILES):
+            for f in (SIGMOID, GELU, RELU, TANH):
+                h_ps[f, i] = bank(4 * (1 - i) + (f + 2) % 4, "h_ps%d%d" % (f, i))[:, 0:P]
+        quantise_x(0)
+        regroup_w(nc.vector.tensor_copy, 0, RELU)
+        regroup_w(nc.scalar.copy, 0, TANH)
+        first_product(0, SIGMOID, 0)
+        first_product(0, GELU, 0)
+        quantise_x(1)
+        first_product(0, SIGMOID, 1)
+        first_product(0, GELU, 1)
+        quantise_w(0, RELU)
+        regroup_w(nc.vector.tensor_copy, 1, SIGMOID)
+        regroup_w(nc.scalar.copy, 1, GELU)
+        quantise_w(0, TANH)
+        for f in (RELU, TANH):
+            for i in range(TOKEN_TILES):
+                first_product(0, f, i)
+        regroup_w(nc.vector.tensor_copy, 1, RELU)
+        regroup_w(nc.scalar.copy, 1, TANH)
+        for f in (SIGMOID, GELU, RELU, TANH):
+            quantise_w(1, f)
+            for i in range(TOKEN_TILES):
+                first_product(1, f, i)
 
         agg_grp = keep.tile([P, D_OUT, PACK], BF16, align_bytes=64)
         agg_codes = keep.tile([P, D_OUT], U32, align_bytes=64)
@@ -158,18 +186,25 @@ def tile_kan_s_kernel(tc, x, W, b, agg, out):
         c_codes = keep.tile([P, TOKEN_TILES, P], U32, align_bytes=64)
         c_scales = keep.tile([P, TOKEN_TILES, P], U8, align_bytes=64)
 
-        def scalar_activations(tokens):
+        def scalar_activations(i):
+            tokens = slice(i * P, (i + 1) * P)
             nc.scalar.activation(
-                out=sig[:, tokens], in_=h_ps[2][:, tokens], func=ACT.Tanh, scale=0.5, bias=half_bias[:, 0:1]
+                out=sig[:, tokens], in_=h_ps[SIGMOID, i], func=ACT.Tanh, scale=0.5, bias=half_bias[:, 0:1]
             )
             nc.scalar.activation(
-                out=act[:, 3, tokens], in_=h_ps[3][:, tokens], func=ACT.Gelu, bias=bias[:, 3:4]
+                out=act[:, GELU, tokens], in_=h_ps[GELU, i], func=ACT.Gelu, bias=bias[:, GELU : GELU + 1]
             )
             nc.scalar.activation(
-                out=act[:, 1, tokens], in_=h_ps[1][:, tokens], func=ACT.Tanh, bias=bias[:, 1:2]
+                out=act[:, SIGMOID, tokens], in_=sig[:, tokens], func=ACT.Identity, scale=0.5, bias=half[:, 0:1]
             )
             nc.scalar.activation(
-                out=act[:, 2, tokens], in_=sig[:, tokens], func=ACT.Identity, scale=0.5, bias=half[:, 0:1]
+                out=act[:, TANH, tokens], in_=h_ps[TANH, i], func=ACT.Tanh, bias=bias[:, TANH : TANH + 1]
+            )
+
+        def relu(i):
+            nc.vector.tensor_scalar(
+                out=act[:, RELU, i * P : (i + 1) * P], in0=h_ps[RELU, i],
+                scalar1=bias[:, RELU : RELU + 1], scalar2=0.0, op0=ALU.add, op1=ALU.max,
             )
 
         def regroup_c(copy, i):
@@ -185,10 +220,8 @@ def tile_kan_s_kernel(tc, x, W, b, agg, out):
             )
 
         for i in range(TOKEN_TILES):
-            scalar_activations(slice(i * P, (i + 1) * P))
-        nc.vector.tensor_scalar(
-            out=act[:, 0, :], in0=h_ps[0][:], scalar1=bias[:, 0:1], scalar2=0.0, op0=ALU.add, op1=ALU.max
-        )
+            scalar_activations(i)
+            relu(i)
         nc.vector.quantize_mx(
             out=agg_codes[:].bitcast(FP8X4),
             scales=agg_scales[:],
@@ -203,9 +236,9 @@ def tile_kan_s_kernel(tc, x, W, b, agg, out):
             out_sb = keep.tile([P, D_OUT], F32, name="out_sb%d" % i)
             for j in range(2):
                 cols = slice(j * HALF_OUT, (j + 1) * HALF_OUT)
-                out_ps = psum.tile([P, HALF_OUT], F32, name="out_ps%d%d" % (i, j), tag="bank%d%d" % (i, j))
+                out_ps = bank(4 * (1 - i) + j, "out_ps%d%d" % (i, j))[:, 0:HALF_OUT]
                 nc.tensor.matmul_mx(
-                    out=out_ps[:],
+                    out=out_ps,
                     lhsT=c_codes[:, i, :].bitcast(FP8X4),
                     lhsT_scale=c_scales[:, i, :],
                     rhs=agg_codes[:, cols].bitcast(FP8X4),
@@ -214,7 +247,7 @@ def tile_kan_s_kernel(tc, x, W, b, agg, out):
                     stop=True,
                 )
                 if j == 1:
-                    nc.vector.tensor_copy(out=out_sb[:, cols], in_=out_ps[:])
+                    nc.vector.tensor_copy(out=out_sb[:, cols], in_=out_ps)
                 else:
-                    nc.scalar.copy(out=out_sb[:, cols], in_=out_ps[:])
+                    nc.scalar.copy(out=out_sb[:, cols], in_=out_ps)
             nc.sync.dma_start(out=out[i * P : (i + 1) * P, :], in_=out_sb[:])

@@ -25,6 +25,8 @@ BANK = 512
 
 FLOPS = 2 * TOKENS * D_IN * BRANCHES + 2 * TOKENS * BRANCHES * D_OUT
 
+EARLY_WARM = 10
+LATE_WARM = 8
 AGG_SCALAR_COLS = 128
 
 
@@ -41,8 +43,25 @@ def tile_kan_s_kernel(tc, x, W, b, agg, out):
         nc.scalar.activation(out=warm[:], in_=zero[:], func=ACT.Gelu)
         b_rows = keep.tile([P, P], BF16)
         nc.vector.memset(b_rows[:], 0.0)
+        warm_src = keep.tile([P, PACK * P], BF16, align_bytes=64)
+        nc.vector.memset(warm_src[:], 0.0)
+
+        warm_codes = keep.tile([P, P], U32, align_bytes=64)
+        warm_scales = keep.tile([P, P], U8, align_bytes=64)
+        nc.vector.quantize_mx(out=warm_codes[:].bitcast(FP8X4), scales=warm_scales[:], in_=warm_src[:])
         pick = keep.tile([P, PACK], BF16)
         nc.vector.tensor_copy(out=pick[:], in_=ident[:, 0:PACK])
+
+        def bank(number, label):
+            tile = psum.tile([P, BANK], F32, name=label, tag="bank%d" % number)
+            return tile
+
+        idle_ps = bank(2, "warm_ps")
+        for n in range(EARLY_WARM):
+            nc.tensor.matmul_mx(
+                out=idle_ps[:, 0:P], lhsT=warm_codes[:].bitcast(FP8X4), lhsT_scale=warm_scales[:],
+                rhs=warm_codes[:].bitcast(FP8X4), rhs_scale=warm_scales[:], start=True, stop=True,
+            )
 
         x_sb = []
         for i in range(TOKEN_TILES):
@@ -77,10 +96,6 @@ def tile_kan_s_kernel(tc, x, W, b, agg, out):
         w_grp = keep.tile([P, D_PASSES, BRANCHES, PACK], BF16, align_bytes=64)
         w_codes = keep.tile([P, D_PASSES, BRANCHES], U32, align_bytes=64)
         w_scales = keep.tile([P, D_PASSES, BRANCHES], U8, align_bytes=64)
-
-        def bank(number, label):
-            tile = psum.tile([P, BANK], F32, name=label, tag="bank%d" % number)
-            return tile
 
         def transpose_x(i):
             x_words = x_sb[i][:].bitcast(F32)
@@ -120,11 +135,11 @@ def tile_kan_s_kernel(tc, x, W, b, agg, out):
 
         h_ps = {}
 
-        def first_product(g, f, i):
+        def first_product(g, f, i=None):
             cols = slice(f * P, (f + 1) * P)
-            tokens = slice(i * P, (i + 1) * P)
+            tokens = slice(0, TOKENS) if i is None else slice(i * P, (i + 1) * P)
             nc.tensor.matmul_mx(
-                out=h_ps[f, i],
+                out=h_ps[f] if i is None else h_ps[f, i],
                 lhsT=w_codes[:, g, cols].bitcast(FP8X4),
                 lhsT_scale=w_scales[:, g, cols],
                 rhs=x_codes[:, g, tokens].bitcast(FP8X4),
@@ -146,9 +161,14 @@ def tile_kan_s_kernel(tc, x, W, b, agg, out):
         quantise_w(0, GELU)
         transpose_x(0)
         transpose_x(1)
-        for i in range(TOKEN_TILES):
-            for f in (SIGMOID, GELU, RELU, TANH):
-                h_ps[f, i] = bank(4 * (1 - i) + (f + 2) % 4, "h_ps%d%d" % (f, i))[:, 0:P]
+        for f in (SIGMOID, GELU):
+            for i in range(TOKEN_TILES):
+                h_ps[f, i] = bank(4 * (1 - i) + f - SIGMOID, "h_ps%d%d" % (f, i))[:, 0:P]
+        for f in (RELU, TANH):
+            h_tile = bank(6 + f, "h_ps%d" % f)
+            for i in range(TOKEN_TILES):
+                h_ps[f, i] = h_tile[:, i * P : (i + 1) * P]
+            h_ps[f] = h_tile[:, 0:TOKENS]
         quantise_x(0)
         regroup_w(nc.vector.tensor_copy, 0, RELU)
         regroup_w(nc.scalar.copy, 0, TANH)
@@ -161,15 +181,23 @@ def tile_kan_s_kernel(tc, x, W, b, agg, out):
         regroup_w(nc.vector.tensor_copy, 1, SIGMOID)
         regroup_w(nc.scalar.copy, 1, GELU)
         quantise_w(0, TANH)
-        for f in (RELU, TANH):
-            for i in range(TOKEN_TILES):
-                first_product(0, f, i)
+        first_product(0, RELU)
+        first_product(0, TANH)
         regroup_w(nc.vector.tensor_copy, 1, RELU)
         regroup_w(nc.scalar.copy, 1, TANH)
-        for f in (SIGMOID, GELU, RELU, TANH):
+        for f in (SIGMOID, GELU):
             quantise_w(1, f)
             for i in range(TOKEN_TILES):
                 first_product(1, f, i)
+        for f in (RELU, TANH):
+            quantise_w(1, f)
+            first_product(1, f)
+        idle_ps = bank(2, "idle_ps")
+        for n in range(LATE_WARM):
+            nc.tensor.matmul_mx(
+                out=idle_ps[:, 0:TOKENS], lhsT=w_codes[:, 1, 0:P].bitcast(FP8X4), lhsT_scale=w_scales[:, 1, 0:P],
+                rhs=x_codes[:, 1, :].bitcast(FP8X4), rhs_scale=x_scales[:, 1, :], start=True, stop=True,
+            )
 
         agg_grp = keep.tile([P, D_OUT, PACK], BF16, align_bytes=64)
         agg_codes = keep.tile([P, D_OUT], U32, align_bytes=64)
@@ -222,12 +250,12 @@ def tile_kan_s_kernel(tc, x, W, b, agg, out):
         for i in range(TOKEN_TILES):
             scalar_activations(i)
             relu(i)
+        regroup_c(nc.vector.tensor_copy, 0)
         nc.vector.quantize_mx(
             out=agg_codes[:].bitcast(FP8X4),
             scales=agg_scales[:],
             in_=agg_grp[:].rearrange("p o t -> p (o t)"),
         )
-        regroup_c(nc.vector.tensor_copy, 0)
         regroup_c(nc.scalar.copy, 1)
         quantise_c(0)
         quantise_c(1)
@@ -236,7 +264,7 @@ def tile_kan_s_kernel(tc, x, W, b, agg, out):
             out_sb = keep.tile([P, D_OUT], F32, name="out_sb%d" % i)
             for j in range(2):
                 cols = slice(j * HALF_OUT, (j + 1) * HALF_OUT)
-                out_ps = bank(4 * (1 - i) + j, "out_ps%d%d" % (i, j))[:, 0:HALF_OUT]
+                out_ps = bank((3, 6)[j] if i == 0 else 4 + j, "out_ps%d%d" % (i, j))[:, 0:HALF_OUT]
                 nc.tensor.matmul_mx(
                     out=out_ps,
                     lhsT=c_codes[:, i, :].bitcast(FP8X4),

@@ -25,8 +25,6 @@ BANK = 512
 
 FLOPS = 2 * TOKENS * D_IN * BRANCHES + 2 * TOKENS * BRANCHES * D_OUT
 
-EARLY_WARM = 10
-LATE_WARM = 8
 AGG_SCALAR_COLS = 128
 
 
@@ -43,25 +41,13 @@ def tile_kan_s_kernel(tc, x, W, b, agg, out):
         nc.scalar.activation(out=warm[:], in_=zero[:], func=ACT.Gelu)
         b_rows = keep.tile([P, P], BF16)
         nc.vector.memset(b_rows[:], 0.0)
-        warm_src = keep.tile([P, PACK * P], BF16, align_bytes=64)
-        nc.vector.memset(warm_src[:], 0.0)
 
-        warm_codes = keep.tile([P, P], U32, align_bytes=64)
-        warm_scales = keep.tile([P, P], U8, align_bytes=64)
-        nc.vector.quantize_mx(out=warm_codes[:].bitcast(FP8X4), scales=warm_scales[:], in_=warm_src[:])
         pick = keep.tile([P, PACK], BF16)
         nc.vector.tensor_copy(out=pick[:], in_=ident[:, 0:PACK])
 
         def bank(number, label):
             tile = psum.tile([P, BANK], F32, name=label, tag="bank%d" % number)
             return tile
-
-        idle_ps = bank(2, "warm_ps")
-        for n in range(EARLY_WARM):
-            nc.tensor.matmul_mx(
-                out=idle_ps[:, 0:P], lhsT=warm_codes[:].bitcast(FP8X4), lhsT_scale=warm_scales[:],
-                rhs=warm_codes[:].bitcast(FP8X4), rhs_scale=warm_scales[:], start=True, stop=True,
-            )
 
         x_sb = []
         for i in range(TOKEN_TILES):
@@ -192,12 +178,6 @@ def tile_kan_s_kernel(tc, x, W, b, agg, out):
         for f in (RELU, TANH):
             quantise_w(1, f)
             first_product(1, f)
-        idle_ps = bank(2, "idle_ps")
-        for n in range(LATE_WARM):
-            nc.tensor.matmul_mx(
-                out=idle_ps[:, 0:TOKENS], lhsT=w_codes[:, 1, 0:P].bitcast(FP8X4), lhsT_scale=w_scales[:, 1, 0:P],
-                rhs=x_codes[:, 1, :].bitcast(FP8X4), rhs_scale=x_scales[:, 1, :], start=True, stop=True,
-            )
 
         agg_grp = keep.tile([P, D_OUT, PACK], BF16, align_bytes=64)
         agg_codes = keep.tile([P, D_OUT], U32, align_bytes=64)

@@ -33,15 +33,15 @@ def tile_kan_s_kernel(tc, x, W, b, agg, out):
     with tc.tile_pool(name="keep", bufs=1) as keep, tc.psum_pool(name="psum", bufs=1) as psum, tc.manual_schedule():
         ident = keep.tile([P, P], F32)
         make_identity(nc, ident[:])
+        b_rows = keep.tile([P, P], BF16)
+        nc.vector.memset(b_rows[:], 0.0)
         zero = keep.tile([P, 1], F32)
         nc.vector.memset(zero[:], 0.0)
         half = keep.tile([P, 1], F32)
         nc.vector.memset(half[:], 0.5)
+
         warm = keep.tile([P, 1], F32)
         nc.scalar.activation(out=warm[:], in_=zero[:], func=ACT.Gelu)
-        b_rows = keep.tile([P, P], BF16)
-        nc.vector.memset(b_rows[:], 0.0)
-
         pick = keep.tile([P, PACK], BF16)
         nc.vector.tensor_copy(out=pick[:], in_=ident[:, 0:PACK])
 
@@ -54,21 +54,14 @@ def tile_kan_s_kernel(tc, x, W, b, agg, out):
             x_tile = keep.tile([P, D_IN], BF16, name="x_sb%d" % i)
             x_sb.append(x_tile)
         w_raw = keep.tile([P, D_PASSES, PACK, BRANCHES], BF16)
-
-        def load_w(g, f):
-            cols = slice(f * P, (f + 2) * P)
+        for step in range(TOKEN_TILES):
+            nc.sync.dma_start(out=x_sb[step][:], in_=x[step * P : (step + 1) * P, :])
+            if step == 0:
+                nc.sync.dma_start(out=b_rows[0:PACK, :], in_=b.rearrange("(f p) -> f p", f=PACK))
             nc.sync.dma_start(
-                out=w_raw[:, g, :, cols],
-                in_=W[g * K_PASS : (g + 1) * K_PASS, cols].rearrange("(p t) c -> p t c", t=PACK),
+                out=w_raw[:, step, :, :],
+                in_=W[step * K_PASS : (step + 1) * K_PASS, :].rearrange("(p t) c -> p t c", t=PACK),
             )
-
-        load_w(0, SIGMOID)
-        nc.sync.dma_start(out=b_rows[0:PACK, :], in_=b.rearrange("(f p) -> f p", f=PACK))
-        for i in range(TOKEN_TILES):
-            nc.sync.dma_start(out=x_sb[i][:], in_=x[i * P : (i + 1) * P, :])
-        load_w(0, RELU)
-        load_w(1, SIGMOID)
-        load_w(1, RELU)
         agg_raw = keep.tile([P, PACK, D_OUT], BF16)
         nc.sync.dma_start(out=agg_raw[:], in_=agg.rearrange("(t p) o -> p t o", t=PACK))
 
@@ -104,15 +97,15 @@ def tile_kan_s_kernel(tc, x, W, b, agg, out):
                     in_=x_grp[:, g, tokens, :].rearrange("p n t -> p (n t)"),
                 )
 
-        def regroup_w(copy, g, f):
-            cols = slice(f * P, (f + 1) * P)
+        def regroup_w(copy, g, f, count=1):
+            cols = slice(f * P, (f + count) * P)
             copy(
                 out=w_grp[:, g, cols, :].rearrange("p (c i) t -> p c t i", i=4),
                 in_=w_raw[:, g, :, cols].rearrange("p t (c i) -> p c t i", i=4),
             )
 
-        def quantise_w(g, f):
-            cols = slice(f * P, (f + 1) * P)
+        def quantise_w(g, f, count=1):
+            cols = slice(f * P, (f + count) * P)
             nc.vector.quantize_mx(
                 out=w_codes[:, g, cols].bitcast(FP8X4),
                 scales=w_scales[:, g, cols],
@@ -121,62 +114,47 @@ def tile_kan_s_kernel(tc, x, W, b, agg, out):
 
         h_ps = {}
 
-        def first_product(g, f, i=None):
+        def first_product(g, f):
             cols = slice(f * P, (f + 1) * P)
-            tokens = slice(0, TOKENS) if i is None else slice(i * P, (i + 1) * P)
             nc.tensor.matmul_mx(
-                out=h_ps[f] if i is None else h_ps[f, i],
+                out=h_ps[f],
                 lhsT=w_codes[:, g, cols].bitcast(FP8X4),
                 lhsT_scale=w_scales[:, g, cols],
-                rhs=x_codes[:, g, tokens].bitcast(FP8X4),
-                rhs_scale=x_scales[:, g, tokens],
+                rhs=x_codes[:, g, :].bitcast(FP8X4),
+                rhs_scale=x_scales[:, g, :],
                 start=(g == 0),
                 stop=(g == D_PASSES - 1),
             )
 
-        bias_ps = bank(7, "bias_ps")[:, 0:PACK]
+        transpose_x(0)
+        bias_ps = bank(4, "bias_ps")[:, 0:PACK]
         nc.tensor.matmul(bias_ps, lhsT=b_rows[:], rhs=pick[:], start=True, stop=True)
         bias = keep.tile([P, PACK], F32)
         half_bias = keep.tile([P, 1], F32)
-
-        regroup_w(nc.vector.tensor_copy, 0, SIGMOID)
-        regroup_w(nc.scalar.copy, 0, GELU)
-        nc.scalar.copy(out=bias[:], in_=bias_ps)
-        nc.scalar.mul(out=half_bias[:], in_=bias[:, SIGMOID : SIGMOID + 1], mul=0.5)
-        quantise_w(0, SIGMOID)
-        quantise_w(0, GELU)
-        transpose_x(0)
-        transpose_x(1)
-        for f in (SIGMOID, GELU):
-            for i in range(TOKEN_TILES):
-                h_ps[f, i] = bank(4 * (1 - i) + f - SIGMOID, "h_ps%d%d" % (f, i))[:, 0:P]
-        for f in (RELU, TANH):
-            h_tile = bank(6 + f, "h_ps%d" % f)
-            for i in range(TOKEN_TILES):
-                h_ps[f, i] = h_tile[:, i * P : (i + 1) * P]
-            h_ps[f] = h_tile[:, 0:TOKENS]
+        nc.vector.tensor_copy(out=bias[:], in_=bias_ps)
+        nc.vector.tensor_scalar(
+            out=half_bias[:], in0=bias_ps[:, SIGMOID : SIGMOID + 1], scalar1=0.5, scalar2=None, op0=ALU.mult
+        )
         quantise_x(0)
-        regroup_w(nc.vector.tensor_copy, 0, RELU)
-        regroup_w(nc.scalar.copy, 0, TANH)
-        first_product(0, SIGMOID, 0)
-        first_product(0, GELU, 0)
+        regroup_w(nc.vector.tensor_copy, 0, RELU, 2)
+        regroup_w(nc.scalar.copy, 0, SIGMOID)
+        regroup_w(nc.scalar.copy, 0, GELU)
+        transpose_x(1)
+        for f in range(PACK):
+            h_ps[f] = bank(4 + f, "h_ps%d" % f)[:, 0:TOKENS]
+        quantise_w(0, SIGMOID)
+        quantise_w(0, RELU, 2)
+        quantise_w(0, GELU)
         quantise_x(1)
-        first_product(0, SIGMOID, 1)
-        first_product(0, GELU, 1)
-        quantise_w(0, RELU)
-        regroup_w(nc.vector.tensor_copy, 1, SIGMOID)
+        for f in (SIGMOID, TANH, GELU, RELU):
+            first_product(0, f)
+        regroup_w(nc.vector.tensor_copy, 1, RELU, 2)
+        regroup_w(nc.scalar.copy, 1, SIGMOID)
         regroup_w(nc.scalar.copy, 1, GELU)
-        quantise_w(0, TANH)
-        first_product(0, RELU)
-        first_product(0, TANH)
-        regroup_w(nc.vector.tensor_copy, 1, RELU)
-        regroup_w(nc.scalar.copy, 1, TANH)
-        for f in (SIGMOID, GELU):
-            quantise_w(1, f)
-            for i in range(TOKEN_TILES):
-                first_product(1, f, i)
-        for f in (RELU, TANH):
-            quantise_w(1, f)
+        quantise_w(1, SIGMOID)
+        quantise_w(1, RELU, 2)
+        quantise_w(1, GELU)
+        for f in (SIGMOID, TANH, GELU, RELU):
             first_product(1, f)
 
         agg_grp = keep.tile([P, D_OUT, PACK], BF16, align_bytes=64)
@@ -188,32 +166,19 @@ def tile_kan_s_kernel(tc, x, W, b, agg, out):
         nc.scalar.copy(out=agg_dst[:, :split], in_=agg_src[:, :split])
         nc.vector.tensor_copy(out=agg_dst[:, split:], in_=agg_src[:, split:])
 
+        def quantise_agg(j):
+            cols = slice(j * HALF_OUT, (j + 1) * HALF_OUT)
+            nc.vector.quantize_mx(
+                out=agg_codes[:, cols].bitcast(FP8X4),
+                scales=agg_scales[:, cols],
+                in_=agg_grp[:, cols, :].rearrange("p o t -> p (o t)"),
+            )
+
         act = keep.tile([P, PACK, TOKENS], BF16)
         sig = keep.tile([P, TOKENS], F32)
         c_grp = keep.tile([P, TOKEN_TILES, P, PACK], BF16, align_bytes=64)
         c_codes = keep.tile([P, TOKEN_TILES, P], U32, align_bytes=64)
         c_scales = keep.tile([P, TOKEN_TILES, P], U8, align_bytes=64)
-
-        def scalar_activations(i):
-            tokens = slice(i * P, (i + 1) * P)
-            nc.scalar.activation(
-                out=sig[:, tokens], in_=h_ps[SIGMOID, i], func=ACT.Tanh, scale=0.5, bias=half_bias[:, 0:1]
-            )
-            nc.scalar.activation(
-                out=act[:, GELU, tokens], in_=h_ps[GELU, i], func=ACT.Gelu, bias=bias[:, GELU : GELU + 1]
-            )
-            nc.scalar.activation(
-                out=act[:, SIGMOID, tokens], in_=sig[:, tokens], func=ACT.Identity, scale=0.5, bias=half[:, 0:1]
-            )
-            nc.scalar.activation(
-                out=act[:, TANH, tokens], in_=h_ps[TANH, i], func=ACT.Tanh, bias=bias[:, TANH : TANH + 1]
-            )
-
-        def relu(i):
-            nc.vector.tensor_scalar(
-                out=act[:, RELU, i * P : (i + 1) * P], in0=h_ps[RELU, i],
-                scalar1=bias[:, RELU : RELU + 1], scalar2=0.0, op0=ALU.add, op1=ALU.max,
-            )
 
         def regroup_c(copy, i):
             copy(
@@ -227,16 +192,18 @@ def tile_kan_s_kernel(tc, x, W, b, agg, out):
                 in_=c_grp[:, i, :, :].rearrange("p n t -> p (n t)"),
             )
 
-        for i in range(TOKEN_TILES):
-            scalar_activations(i)
-            relu(i)
-        regroup_c(nc.vector.tensor_copy, 0)
-        nc.vector.quantize_mx(
-            out=agg_codes[:].bitcast(FP8X4),
-            scales=agg_scales[:],
-            in_=agg_grp[:].rearrange("p o t -> p (o t)"),
+        nc.scalar.activation(out=sig[:], in_=h_ps[SIGMOID], func=ACT.Tanh, scale=0.5, bias=half_bias[:, 0:1])
+        nc.scalar.activation(out=act[:, TANH, :], in_=h_ps[TANH], func=ACT.Tanh, bias=bias[:, TANH : TANH + 1])
+        nc.scalar.activation(out=act[:, SIGMOID, :], in_=sig[:], func=ACT.Identity, scale=0.5, bias=half[:, 0:1])
+        nc.scalar.activation(out=act[:, GELU, :], in_=h_ps[GELU], func=ACT.Gelu, bias=bias[:, GELU : GELU + 1])
+        nc.vector.tensor_scalar(
+            out=act[:, RELU, :], in0=h_ps[RELU], scalar1=bias[:, RELU : RELU + 1], scalar2=0.0,
+            op0=ALU.add, op1=ALU.max,
         )
+        quantise_agg(0)
+        regroup_c(nc.vector.tensor_copy, 0)
         regroup_c(nc.scalar.copy, 1)
+        quantise_agg(1)
         quantise_c(0)
         quantise_c(1)
 
@@ -244,7 +211,7 @@ def tile_kan_s_kernel(tc, x, W, b, agg, out):
             out_sb = keep.tile([P, D_OUT], F32, name="out_sb%d" % i)
             for j in range(2):
                 cols = slice(j * HALF_OUT, (j + 1) * HALF_OUT)
-                out_ps = bank((3, 6)[j] if i == 0 else 4 + j, "out_ps%d%d" % (i, j))[:, 0:HALF_OUT]
+                out_ps = bank(2 * i + j, "out_ps%d%d" % (i, j))[:, 0:HALF_OUT]
                 nc.tensor.matmul_mx(
                     out=out_ps,
                     lhsT=c_codes[:, i, :].bitcast(FP8X4),

@@ -25,7 +25,8 @@ BANK = 512
 
 FLOPS = 2 * TOKENS * D_IN * BRANCHES + 2 * TOKENS * BRANCHES * D_OUT
 
-AGG_SCALAR_COLS = 128
+LATE_WARM = 3
+AGG_SCALAR_COLS = 192
 
 
 def tile_kan_s_kernel(tc, x, W, b, agg, out):
@@ -76,14 +77,14 @@ def tile_kan_s_kernel(tc, x, W, b, agg, out):
         w_codes = keep.tile([P, D_PASSES, BRANCHES], U32, align_bytes=64)
         w_scales = keep.tile([P, D_PASSES, BRANCHES], U8, align_bytes=64)
 
-        def transpose_x(i):
+        def transpose_x(i, copies):
             x_words = x_sb[i][:].bitcast(F32)
             for g in range(D_PASSES):
                 xt = bank(2 * i + g, "xt%d%d" % (i, g))[:, 0 : 2 * P].rearrange("p (u n) -> p u n", u=2)
                 for u in range(2):
                     first = 2 * P * g + u
                     nc.tensor.transpose(xt[:, u, :], x_words[:, first : 2 * P * (g + 1) : 2], ident[:])
-                nc.scalar.copy(
+                copies[g](
                     out=x_grp_words[:, g, i * P : (i + 1) * P, :],
                     in_=xt.rearrange("p u n -> p n u"),
                 )
@@ -126,7 +127,7 @@ def tile_kan_s_kernel(tc, x, W, b, agg, out):
                 stop=(g == D_PASSES - 1),
             )
 
-        transpose_x(0)
+        transpose_x(0, (nc.scalar.copy, nc.vector.tensor_copy))
         bias_ps = bank(4, "bias_ps")[:, 0:PACK]
         nc.tensor.matmul(bias_ps, lhsT=b_rows[:], rhs=pick[:], start=True, stop=True)
         bias = keep.tile([P, PACK], F32)
@@ -135,11 +136,11 @@ def tile_kan_s_kernel(tc, x, W, b, agg, out):
         nc.vector.tensor_scalar(
             out=half_bias[:], in0=bias_ps[:, SIGMOID : SIGMOID + 1], scalar1=0.5, scalar2=None, op0=ALU.mult
         )
-        quantise_x(0)
         regroup_w(nc.vector.tensor_copy, 0, RELU, 2)
+        quantise_x(0)
         regroup_w(nc.scalar.copy, 0, SIGMOID)
         regroup_w(nc.scalar.copy, 0, GELU)
-        transpose_x(1)
+        transpose_x(1, (nc.scalar.copy, nc.scalar.copy))
         for f in range(PACK):
             h_ps[f] = bank(4 + f, "h_ps%d" % f)[:, 0:TOKENS]
         quantise_w(0, SIGMOID)
@@ -154,8 +155,14 @@ def tile_kan_s_kernel(tc, x, W, b, agg, out):
         quantise_w(1, SIGMOID)
         quantise_w(1, RELU, 2)
         quantise_w(1, GELU)
-        for f in (SIGMOID, TANH, GELU, RELU):
+        for f in (SIGMOID, TANH, RELU, GELU):
             first_product(1, f)
+        idle_ps = bank(0, "idle_ps")
+        for n in range(LATE_WARM):
+            nc.tensor.matmul_mx(
+                out=idle_ps[:, 0:TOKENS], lhsT=w_codes[:, 1, 0:P].bitcast(FP8X4), lhsT_scale=w_scales[:, 1, 0:P],
+                rhs=x_codes[:, 1, :].bitcast(FP8X4), rhs_scale=x_scales[:, 1, :], start=True, stop=True,
+            )
 
         agg_grp = keep.tile([P, D_OUT, PACK], BF16, align_bytes=64)
         agg_codes = keep.tile([P, D_OUT], U32, align_bytes=64)
@@ -195,7 +202,11 @@ def tile_kan_s_kernel(tc, x, W, b, agg, out):
         nc.scalar.activation(out=sig[:], in_=h_ps[SIGMOID], func=ACT.Tanh, scale=0.5, bias=half_bias[:, 0:1])
         nc.scalar.activation(out=act[:, TANH, :], in_=h_ps[TANH], func=ACT.Tanh, bias=bias[:, TANH : TANH + 1])
         nc.scalar.activation(out=act[:, SIGMOID, :], in_=sig[:], func=ACT.Identity, scale=0.5, bias=half[:, 0:1])
-        nc.scalar.activation(out=act[:, GELU, :], in_=h_ps[GELU], func=ACT.Gelu, bias=bias[:, GELU : GELU + 1])
+        for i in range(TOKEN_TILES):
+            tokens = slice(i * P, (i + 1) * P)
+            nc.scalar.activation(
+                out=act[:, GELU, tokens], in_=h_ps[GELU][:, tokens], func=ACT.Gelu, bias=bias[:, GELU : GELU + 1]
+            )
         nc.vector.tensor_scalar(
             out=act[:, RELU, :], in0=h_ps[RELU], scalar1=bias[:, RELU : RELU + 1], scalar2=0.0,
             op0=ALU.add, op1=ALU.max,
@@ -225,4 +236,4 @@ def tile_kan_s_kernel(tc, x, W, b, agg, out):
                     nc.vector.tensor_copy(out=out_sb[:, cols], in_=out_ps)
                 else:
                     nc.scalar.copy(out=out_sb[:, cols], in_=out_ps)
-            nc.sync.dma_start(out=out[i * P : (i + 1) * P, :], in_=out_sb[:])
+                nc.sync.dma_start(out=out[i * P : (i + 1) * P, cols], in_=out_sb[:, cols])

@@ -26,7 +26,7 @@ BANK = 512
 FLOPS = 2 * TOKENS * D_IN * BRANCHES + 2 * TOKENS * BRANCHES * D_OUT
 
 LATE_WARM = 3
-AGG_SCALAR_COLS = 192
+AGG_SCALAR_COLS = 128
 
 
 def tile_kan_s_kernel(tc, x, W, b, agg, out):
@@ -132,10 +132,8 @@ def tile_kan_s_kernel(tc, x, W, b, agg, out):
         nc.tensor.matmul(bias_ps, lhsT=b_rows[:], rhs=pick[:], start=True, stop=True)
         bias = keep.tile([P, PACK], F32)
         half_bias = keep.tile([P, 1], F32)
-        nc.vector.tensor_copy(out=bias[:], in_=bias_ps)
-        nc.vector.tensor_scalar(
-            out=half_bias[:], in0=bias_ps[:, SIGMOID : SIGMOID + 1], scalar1=0.5, scalar2=None, op0=ALU.mult
-        )
+        nc.scalar.copy(out=bias[:], in_=bias_ps)
+        nc.scalar.mul(out=half_bias[:], in_=bias_ps[:, SIGMOID : SIGMOID + 1], mul=0.5)
         regroup_w(nc.vector.tensor_copy, 0, RELU, 2)
         quantise_x(0)
         regroup_w(nc.scalar.copy, 0, SIGMOID)
@@ -143,9 +141,8 @@ def tile_kan_s_kernel(tc, x, W, b, agg, out):
         transpose_x(1, (nc.scalar.copy, nc.scalar.copy))
         for f in range(PACK):
             h_ps[f] = bank(4 + f, "h_ps%d" % f)[:, 0:TOKENS]
-        quantise_w(0, SIGMOID)
         quantise_w(0, RELU, 2)
-        quantise_w(0, GELU)
+        quantise_w(0, SIGMOID, 2)
         quantise_x(1)
         for f in (SIGMOID, TANH, GELU, RELU):
             first_product(0, f)

@@ -128,17 +128,17 @@ def tile_kan_s_kernel(tc, x, W, b, agg, out):
             )
 
         transpose_x(0, (nc.scalar.copy, nc.vector.tensor_copy))
+        regroup_w(nc.vector.tensor_copy, 0, RELU, 2)
+        quantise_x(0)
+        regroup_w(nc.scalar.copy, 0, SIGMOID)
+        regroup_w(nc.scalar.copy, 0, GELU)
+        transpose_x(1, (nc.scalar.copy, nc.scalar.copy))
         bias_ps = bank(4, "bias_ps")[:, 0:PACK]
         nc.tensor.matmul(bias_ps, lhsT=b_rows[:], rhs=pick[:], start=True, stop=True)
         bias = keep.tile([P, PACK], F32)
         half_bias = keep.tile([P, 1], F32)
         nc.scalar.copy(out=bias[:], in_=bias_ps)
         nc.scalar.mul(out=half_bias[:], in_=bias_ps[:, SIGMOID : SIGMOID + 1], mul=0.5)
-        regroup_w(nc.vector.tensor_copy, 0, RELU, 2)
-        quantise_x(0)
-        regroup_w(nc.scalar.copy, 0, SIGMOID)
-        regroup_w(nc.scalar.copy, 0, GELU)
-        transpose_x(1, (nc.scalar.copy, nc.scalar.copy))
         for f in range(PACK):
             h_ps[f] = bank(4 + f, "h_ps%d" % f)[:, 0:TOKENS]
         quantise_w(0, RELU, 2)

@@ -26,7 +26,7 @@ BANK = 512
 FLOPS = 2 * TOKENS * D_IN * BRANCHES + 2 * TOKENS * BRANCHES * D_OUT
 
 LATE_WARM = 3
-AGG_SCALAR_COLS = 128
+AGG_SCALAR_COLS = 160
 
 
 def tile_kan_s_kernel(tc, x, W, b, agg, out):
@@ -51,18 +51,16 @@ def tile_kan_s_kernel(tc, x, W, b, agg, out):
             return tile
 
         x_sb = []
-        for i in range(TOKEN_TILES):
-            x_tile = keep.tile([P, D_IN], BF16, name="x_sb%d" % i)
+        for g in range(D_PASSES):
+            x_tile = keep.tile([P, TOKEN_TILES, K_PASS], BF16, name="x_sb%d" % g)
             x_sb.append(x_tile)
         w_raw = keep.tile([P, D_PASSES, PACK, BRANCHES], BF16)
-        for step in range(TOKEN_TILES):
-            nc.sync.dma_start(out=x_sb[step][:], in_=x[step * P : (step + 1) * P, :])
-            if step == 0:
+        for g in range(D_PASSES):
+            rows = slice(g * K_PASS, (g + 1) * K_PASS)
+            nc.sync.dma_start(out=x_sb[g][:], in_=x[:, rows].rearrange("(i p) k -> p i k", p=P))
+            if g == 0:
                 nc.sync.dma_start(out=b_rows[0:PACK, :], in_=b.rearrange("(f p) -> f p", f=PACK))
-            nc.sync.dma_start(
-                out=w_raw[:, step, :, :],
-                in_=W[step * K_PASS : (step + 1) * K_PASS, :].rearrange("(p t) c -> p t c", t=PACK),
-            )
+            nc.sync.dma_start(out=w_raw[:, g, :, :], in_=W[rows, :].rearrange("(p t) c -> p t c", t=PACK))
         agg_raw = keep.tile([P, PACK, D_OUT], BF16)
         nc.sync.dma_start(out=agg_raw[:], in_=agg.rearrange("(t p) o -> p t o", t=PACK))
 
@@ -77,26 +75,23 @@ def tile_kan_s_kernel(tc, x, W, b, agg, out):
         w_codes = keep.tile([P, D_PASSES, BRANCHES], U32, align_bytes=64)
         w_scales = keep.tile([P, D_PASSES, BRANCHES], U8, align_bytes=64)
 
-        def transpose_x(i, copies):
-            x_words = x_sb[i][:].bitcast(F32)
-            for g in range(D_PASSES):
-                xt = bank(2 * i + g, "xt%d%d" % (i, g))[:, 0 : 2 * P].rearrange("p (u n) -> p u n", u=2)
+        def transpose_x(g, copies):
+            for i in range(TOKEN_TILES):
+                words = x_sb[g][:, i, :].bitcast(F32)
+                xt = bank(2 * g + i, "xt%d%d" % (g, i))[:, 0 : 2 * P].rearrange("p (u n) -> p u n", u=2)
                 for u in range(2):
-                    first = 2 * P * g + u
-                    nc.tensor.transpose(xt[:, u, :], x_words[:, first : 2 * P * (g + 1) : 2], ident[:])
-                copies[g](
+                    nc.tensor.transpose(xt[:, u, :], words[:, u : 2 * P : 2], ident[:])
+                copies[i](
                     out=x_grp_words[:, g, i * P : (i + 1) * P, :],
                     in_=xt.rearrange("p u n -> p n u"),
                 )
 
-        def quantise_x(i):
-            tokens = slice(i * P, (i + 1) * P)
-            for g in range(D_PASSES):
-                nc.vector.quantize_mx(
-                    out=x_codes[:, g, tokens].bitcast(FP8X4),
-                    scales=x_scales[:, g, tokens],
-                    in_=x_grp[:, g, tokens, :].rearrange("p n t -> p (n t)"),
-                )
+        def quantise_x(g):
+            nc.vector.quantize_mx(
+                out=x_codes[:, g, :].bitcast(FP8X4),
+                scales=x_scales[:, g, :],
+                in_=x_grp[:, g, :, :].rearrange("p n t -> p (n t)"),
+            )
 
         def regroup_w(copy, g, f, count=1):
             cols = slice(f * P, (f + count) * P)
@@ -143,10 +138,10 @@ def tile_kan_s_kernel(tc, x, W, b, agg, out):
             h_ps[f] = bank(4 + f, "h_ps%d" % f)[:, 0:TOKENS]
         quantise_w(0, RELU, 2)
         quantise_w(0, SIGMOID, 2)
-        quantise_x(1)
-        for f in (SIGMOID, TANH, GELU, RELU):
+        for f in (TANH, RELU, SIGMOID, GELU):
             first_product(0, f)
         regroup_w(nc.vector.tensor_copy, 1, RELU, 2)
+        quantise_x(1)
         regroup_w(nc.scalar.copy, 1, SIGMOID)
         regroup_w(nc.scalar.copy, 1, GELU)
         quantise_w(1, SIGMOID)
@@ -186,7 +181,8 @@ def tile_kan_s_kernel(tc, x, W, b, agg, out):
 
         def regroup_c(copy, i):
             copy(
-                out=c_grp[:, i, :, :], in_=act[:, :, i * P : (i + 1) * P].rearrange("p t n -> p n t")
+                out=c_grp[:, i, :, :].rearrange("p (c i) t -> p c t i", i=4),
+                in_=act[:, :, i * P : (i + 1) * P].rearrange("p t (c i) -> p c t i", i=4),
             )
 
         def quantise_c(i):

@@ -25,9 +25,6 @@ BANK = 512
 
 FLOPS = 2 * TOKENS * D_IN * BRANCHES + 2 * TOKENS * BRANCHES * D_OUT
 
-LATE_WARM = 3
-AGG_SCALAR_COLS = 160
-
 
 def tile_kan_s_kernel(tc, x, W, b, agg, out):
     nc = tc.nc
@@ -43,26 +40,46 @@ def tile_kan_s_kernel(tc, x, W, b, agg, out):
 
         warm = keep.tile([P, 1], F32)
         nc.scalar.activation(out=warm[:], in_=zero[:], func=ACT.Gelu)
-        pick = keep.tile([P, PACK], BF16)
-        nc.vector.tensor_copy(out=pick[:], in_=ident[:, 0:PACK])
+        ident_bf = keep.tile([P, P], BF16)
+        nc.vector.tensor_copy(out=ident_bf[:], in_=ident[:])
 
         def bank(number, label):
             tile = psum.tile([P, BANK], F32, name=label, tag="bank%d" % number)
             return tile
 
-        x_sb = []
+        def bank_bf16(number, label):
+            tile = psum.tile([P, 2 * BANK], BF16, name=label, tag="bank%d" % number)
+            return tile
+
+        x_sb = {}
         for g in range(D_PASSES):
-            x_tile = keep.tile([P, TOKEN_TILES, K_PASS], BF16, name="x_sb%d" % g)
-            x_sb.append(x_tile)
+            for i in range(TOKEN_TILES):
+                x_tile = keep.tile([P, K_PASS], BF16, name="x_sb%d%d" % (g, i))
+                x_sb[g, i] = x_tile
         w_raw = keep.tile([P, D_PASSES, PACK, BRANCHES], BF16)
-        for g in range(D_PASSES):
-            rows = slice(g * K_PASS, (g + 1) * K_PASS)
-            nc.sync.dma_start(out=x_sb[g][:], in_=x[:, rows].rearrange("(i p) k -> p i k", p=P))
-            if g == 0:
-                nc.sync.dma_start(out=b_rows[0:PACK, :], in_=b.rearrange("(f p) -> f p", f=PACK))
-            nc.sync.dma_start(out=w_raw[:, g, :, :], in_=W[rows, :].rearrange("(p t) c -> p t c", t=PACK))
         agg_raw = keep.tile([P, PACK, D_OUT], BF16)
-        nc.sync.dma_start(out=agg_raw[:], in_=agg.rearrange("(t p) o -> p t o", t=PACK))
+
+        def load_x(g, i):
+            nc.sync.dma_start(out=x_sb[g, i][:], in_=x[i * P : (i + 1) * P, g * K_PASS : (g + 1) * K_PASS])
+
+        def load_b():
+            nc.sync.dma_start(out=b_rows[0:PACK, :], in_=b.rearrange("(f p) -> f p", f=PACK))
+
+        def load_w(g):
+            rows = slice(g * K_PASS, (g + 1) * K_PASS)
+            nc.sync.dma_start(out=w_raw[:, g, :, :], in_=W[rows, :].rearrange("(p t) c -> p t c", t=PACK))
+
+        def load_agg():
+            nc.sync.dma_start(out=agg_raw[:], in_=agg.rearrange("(t p) o -> p t o", t=PACK))
+
+        load_w(0)
+        load_x(0, 0)
+        load_x(0, 1)
+        load_b()
+        load_x(1, 0)
+        load_x(1, 1)
+        load_w(1)
+        load_agg()
 
         x_grp = keep.tile([P, D_PASSES, TOKENS, PACK], BF16, align_bytes=64)
         x_grp_words = (
@@ -74,23 +91,33 @@ def tile_kan_s_kernel(tc, x, W, b, agg, out):
         w_grp = keep.tile([P, D_PASSES, BRANCHES, PACK], BF16, align_bytes=64)
         w_codes = keep.tile([P, D_PASSES, BRANCHES], U32, align_bytes=64)
         w_scales = keep.tile([P, D_PASSES, BRANCHES], U8, align_bytes=64)
+        agg_grp = keep.tile([P, D_OUT, PACK], BF16, align_bytes=64)
+        agg_codes = keep.tile([P, D_OUT], U32, align_bytes=64)
+        agg_scales = keep.tile([P, D_OUT], U8, align_bytes=64)
+        act = keep.tile([P, PACK, TOKENS], BF16)
+        sig = keep.tile([P, TOKENS], F32)
+        c_grp = keep.tile([P, TOKEN_TILES, P, PACK], BF16, align_bytes=64)
+        c_codes = keep.tile([P, TOKEN_TILES, P], U32, align_bytes=64)
+        c_scales = keep.tile([P, TOKEN_TILES, P], U8, align_bytes=64)
+        bias = keep.tile([P, PACK], F32)
+        half_bias = keep.tile([P, 1], F32)
 
-        def transpose_x(g, copies):
-            for i in range(TOKEN_TILES):
-                words = x_sb[g][:, i, :].bitcast(F32)
-                xt = bank(2 * g + i, "xt%d%d" % (g, i))[:, 0 : 2 * P].rearrange("p (u n) -> p u n", u=2)
-                for u in range(2):
-                    nc.tensor.transpose(xt[:, u, :], words[:, u : 2 * P : 2], ident[:])
-                copies[i](
-                    out=x_grp_words[:, g, i * P : (i + 1) * P, :],
-                    in_=xt.rearrange("p u n -> p n u"),
-                )
+        scalar = nc.scalar.copy
+        vector = nc.vector.tensor_copy
 
-        def quantise_x(g):
+        def transpose_x(g, i, copy):
+            words = x_sb[g, i][:].bitcast(F32)
+            xt = bank(2 * g + i, "xt%d%d" % (g, i))[:, 0 : 2 * P].rearrange("p (u n) -> p u n", u=2)
+            for u in range(2):
+                nc.tensor.transpose(xt[:, u, :], words[:, u : 2 * P : 2], ident[:])
+            copy(out=x_grp_words[:, g, i * P : (i + 1) * P, :], in_=xt.rearrange("p u n -> p n u"))
+
+        def quantise_x(g, i, count=1):
+            tokens = slice(i * P, (i + count) * P)
             nc.vector.quantize_mx(
-                out=x_codes[:, g, :].bitcast(FP8X4),
-                scales=x_scales[:, g, :],
-                in_=x_grp[:, g, :, :].rearrange("p n t -> p (n t)"),
+                out=x_codes[:, g, tokens].bitcast(FP8X4),
+                scales=x_scales[:, g, tokens],
+                in_=x_grp[:, g, tokens, :].rearrange("p n t -> p (n t)"),
             )
 
         def regroup_w(copy, g, f, count=1):
@@ -110,79 +137,56 @@ def tile_kan_s_kernel(tc, x, W, b, agg, out):
 
         h_ps = {}
 
-        def first_product(g, f):
-            cols = slice(f * P, (f + 1) * P)
-            nc.tensor.matmul_mx(
-                out=h_ps[f],
-                lhsT=w_codes[:, g, cols].bitcast(FP8X4),
-                lhsT_scale=w_scales[:, g, cols],
-                rhs=x_codes[:, g, :].bitcast(FP8X4),
-                rhs_scale=x_scales[:, g, :],
-                start=(g == 0),
-                stop=(g == D_PASSES - 1),
-            )
+        def first_product(g, *functions):
+            for f in functions:
+                if g == 0:
+                    h_ps[f] = bank(4 + f, "h_ps%d" % f)[:, 0:TOKENS]
+                cols = slice(f * P, (f + 1) * P)
+                nc.tensor.matmul_mx(
+                    out=h_ps[f],
+                    lhsT=w_codes[:, g, cols].bitcast(FP8X4),
+                    lhsT_scale=w_scales[:, g, cols],
+                    rhs=x_codes[:, g, :].bitcast(FP8X4),
+                    rhs_scale=x_scales[:, g, :],
+                    start=(g == 0),
+                    stop=(g == D_PASSES - 1),
+                )
 
-        transpose_x(0, (nc.scalar.copy, nc.vector.tensor_copy))
-        regroup_w(nc.vector.tensor_copy, 0, RELU, 2)
-        quantise_x(0)
-        regroup_w(nc.scalar.copy, 0, SIGMOID)
-        regroup_w(nc.scalar.copy, 0, GELU)
-        transpose_x(1, (nc.scalar.copy, nc.scalar.copy))
-        bias_ps = bank(4, "bias_ps")[:, 0:PACK]
-        nc.tensor.matmul(bias_ps, lhsT=b_rows[:], rhs=pick[:], start=True, stop=True)
-        bias = keep.tile([P, PACK], F32)
-        half_bias = keep.tile([P, 1], F32)
-        nc.scalar.copy(out=bias[:], in_=bias_ps)
-        nc.scalar.mul(out=half_bias[:], in_=bias_ps[:, SIGMOID : SIGMOID + 1], mul=0.5)
-        for f in range(PACK):
-            h_ps[f] = bank(4 + f, "h_ps%d" % f)[:, 0:TOKENS]
-        quantise_w(0, RELU, 2)
-        quantise_w(0, SIGMOID, 2)
-        for f in (TANH, RELU, SIGMOID, GELU):
-            first_product(0, f)
-        regroup_w(nc.vector.tensor_copy, 1, RELU, 2)
-        quantise_x(1)
-        regroup_w(nc.scalar.copy, 1, SIGMOID)
-        regroup_w(nc.scalar.copy, 1, GELU)
-        quantise_w(1, SIGMOID)
-        quantise_w(1, RELU, 2)
-        quantise_w(1, GELU)
-        for f in (SIGMOID, TANH, RELU, GELU):
-            first_product(1, f)
-        idle_ps = bank(0, "idle_ps")
-        for n in range(LATE_WARM):
-            nc.tensor.matmul_mx(
-                out=idle_ps[:, 0:TOKENS], lhsT=w_codes[:, 1, 0:P].bitcast(FP8X4), lhsT_scale=w_scales[:, 1, 0:P],
-                rhs=x_codes[:, 1, :].bitcast(FP8X4), rhs_scale=x_scales[:, 1, :], start=True, stop=True,
-            )
+        def bias_columns():
+            bias_ps = bank(0, "bias_ps")[:, 0:PACK]
+            nc.tensor.matmul(bias_ps, lhsT=b_rows[:], rhs=ident_bf[:, 0:PACK], start=True, stop=True)
+            nc.scalar.copy(out=bias[:], in_=bias_ps)
+            nc.scalar.mul(out=half_bias[:], in_=bias_ps[:, SIGMOID : SIGMOID + 1], mul=0.5)
 
-        agg_grp = keep.tile([P, D_OUT, PACK], BF16, align_bytes=64)
-        agg_codes = keep.tile([P, D_OUT], U32, align_bytes=64)
-        agg_scales = keep.tile([P, D_OUT], U8, align_bytes=64)
-        agg_src = agg_raw[:].rearrange("p t (c i) -> p c t i", i=4)
-        agg_dst = agg_grp[:].rearrange("p (c i) t -> p c t i", i=4)
-        split = AGG_SCALAR_COLS // 4
-        nc.scalar.copy(out=agg_dst[:, :split], in_=agg_src[:, :split])
-        nc.vector.tensor_copy(out=agg_dst[:, split:], in_=agg_src[:, split:])
+        def bias_columns_v():
+            bias_ps = bank(0, "bias_ps")[:, 0:PACK]
+            nc.tensor.matmul(bias_ps, lhsT=b_rows[:], rhs=ident_bf[:, 0:PACK], start=True, stop=True)
+            nc.vector.tensor_copy(out=bias[:], in_=bias_ps)
+            nc.vector.tensor_scalar(out=half_bias[:], in0=bias_ps[:, SIGMOID : SIGMOID + 1], scalar1=0.5, scalar2=None, op0=ALU.mult)
 
-        def quantise_agg(j):
-            cols = slice(j * HALF_OUT, (j + 1) * HALF_OUT)
-            nc.vector.quantize_mx(
-                out=agg_codes[:, cols].bitcast(FP8X4),
-                scales=agg_scales[:, cols],
-                in_=agg_grp[:, cols, :].rearrange("p o t -> p (o t)"),
-            )
-
-        act = keep.tile([P, PACK, TOKENS], BF16)
-        sig = keep.tile([P, TOKENS], F32)
-        c_grp = keep.tile([P, TOKEN_TILES, P, PACK], BF16, align_bytes=64)
-        c_codes = keep.tile([P, TOKEN_TILES, P], U32, align_bytes=64)
-        c_scales = keep.tile([P, TOKEN_TILES, P], U8, align_bytes=64)
-
-        def regroup_c(copy, i):
+        def regroup_agg(copy, first, last):
             copy(
-                out=c_grp[:, i, :, :].rearrange("p (c i) t -> p c t i", i=4),
-                in_=act[:, :, i * P : (i + 1) * P].rearrange("p t (c i) -> p c t i", i=4),
+                out=agg_grp[:, first:last, :].rearrange("p (c i) t -> p c t i", i=4),
+                in_=agg_raw[:, :, first:last].rearrange("p t (c i) -> p c t i", i=4),
+            )
+
+        def interleave(number, label, dst, src):
+            n = dst.shape[1]
+            ps = bank_bf16(number, label)[:, 0 : 4 * n]
+            nc.tensor.matmul(ps.rearrange("p (c t) -> p c t", t=PACK), lhsT=ident_bf[:], rhs=src.rearrange("p t c -> p c t"), start=True, stop=True)
+            return ps
+
+        def quantise_agg(first, last):
+            nc.vector.quantize_mx(
+                out=agg_codes[:, first:last].bitcast(FP8X4),
+                scales=agg_scales[:, first:last],
+                in_=agg_grp[:, first:last, :].rearrange("p o t -> p (o t)"),
+            )
+
+        def regroup_c(copy, i, a=0, z=P):
+            copy(
+                out=c_grp[:, i, a:z, :].rearrange("p (c i) t -> p c t i", i=4),
+                in_=act[:, :, i * P + a : i * P + z].rearrange("p t (c i) -> p c t i", i=4),
             )
 
         def quantise_c(i):
@@ -192,41 +196,87 @@ def tile_kan_s_kernel(tc, x, W, b, agg, out):
                 in_=c_grp[:, i, :, :].rearrange("p n t -> p (n t)"),
             )
 
-        nc.scalar.activation(out=sig[:], in_=h_ps[SIGMOID], func=ACT.Tanh, scale=0.5, bias=half_bias[:, 0:1])
-        nc.scalar.activation(out=act[:, TANH, :], in_=h_ps[TANH], func=ACT.Tanh, bias=bias[:, TANH : TANH + 1])
-        nc.scalar.activation(out=act[:, SIGMOID, :], in_=sig[:], func=ACT.Identity, scale=0.5, bias=half[:, 0:1])
-        for i in range(TOKEN_TILES):
-            tokens = slice(i * P, (i + 1) * P)
-            nc.scalar.activation(
-                out=act[:, GELU, tokens], in_=h_ps[GELU][:, tokens], func=ACT.Gelu, bias=bias[:, GELU : GELU + 1]
-            )
-        nc.vector.tensor_scalar(
-            out=act[:, RELU, :], in0=h_ps[RELU], scalar1=bias[:, RELU : RELU + 1], scalar2=0.0,
-            op0=ALU.add, op1=ALU.max,
-        )
-        quantise_agg(0)
-        regroup_c(nc.vector.tensor_copy, 0)
-        regroup_c(nc.scalar.copy, 1)
-        quantise_agg(1)
-        quantise_c(0)
-        quantise_c(1)
+        def sigmoid_tanh(first=0, last=TOKENS):
+            nc.scalar.activation(out=sig[:, first:last], in_=h_ps[SIGMOID][:, first:last], func=ACT.Tanh, scale=0.5, bias=half_bias[:, 0:1])
 
-        for i in range(TOKEN_TILES):
-            out_sb = keep.tile([P, D_OUT], F32, name="out_sb%d" % i)
-            for j in range(2):
-                cols = slice(j * HALF_OUT, (j + 1) * HALF_OUT)
-                out_ps = bank(2 * i + j, "out_ps%d%d" % (i, j))[:, 0:HALF_OUT]
+        def sigmoid_end(engine, first=0, last=TOKENS):
+            engine.tensor_scalar(out=act[:, SIGMOID, first:last], in0=sig[:, first:last], scalar1=0.5, scalar2=0.5, op0=ALU.mult, op1=ALU.add)
+
+        def activate(f, func, first=0, last=TOKENS):
+            nc.scalar.activation(out=act[:, f, first:last], in_=h_ps[f][:, first:last], func=func, bias=bias[:, f : f + 1])
+
+        def relu():
+            nc.vector.tensor_scalar(
+                out=act[:, RELU, :], in0=h_ps[RELU], scalar1=bias[:, RELU : RELU + 1], scalar2=0.0,
+                op0=ALU.add, op1=ALU.max,
+            )
+
+        def stand_in(count, first=0):
+            idle_ps = bank(0, "idle_ps")
+            for n in range(count):
                 nc.tensor.matmul_mx(
-                    out=out_ps,
-                    lhsT=c_codes[:, i, :].bitcast(FP8X4),
-                    lhsT_scale=c_scales[:, i, :],
-                    rhs=agg_codes[:, cols].bitcast(FP8X4),
-                    rhs_scale=agg_scales[:, cols],
-                    start=True,
-                    stop=True,
+                    out=idle_ps[:, 0:TOKENS], lhsT=w_codes[:, 1, 0:P].bitcast(FP8X4), lhsT_scale=w_scales[:, 1, 0:P],
+                    rhs=x_codes[:, 1, :].bitcast(FP8X4), rhs_scale=x_scales[:, 1, :], start=True, stop=True,
                 )
-                if j == 1:
-                    nc.vector.tensor_copy(out=out_sb[:, cols], in_=out_ps)
-                else:
-                    nc.scalar.copy(out=out_sb[:, cols], in_=out_ps)
-                nc.sync.dma_start(out=out[i * P : (i + 1) * P, cols], in_=out_sb[:, cols])
+
+        out_sb = {}
+        for i in range(TOKEN_TILES):
+            out_tile = keep.tile([P, D_OUT], F32, name="out_sb%d" % i)
+            out_sb[i] = out_tile
+
+        def second_product(i, first, last, copy, number):
+            out_ps = bank(number, "out_ps%d_%d" % (i, first))[:, 0 : last - first]
+            nc.tensor.matmul_mx(
+                out=out_ps,
+                lhsT=c_codes[:, i, :].bitcast(FP8X4),
+                lhsT_scale=c_scales[:, i, :],
+                rhs=agg_codes[:, first:last].bitcast(FP8X4),
+                rhs_scale=agg_scales[:, first:last],
+                start=True,
+                stop=True,
+            )
+            copy(out=out_sb[i][:, first:last], in_=out_ps)
+            nc.sync.dma_start(out=out[i * P : (i + 1) * P, first:last], in_=out_sb[i][:, first:last])
+
+        regroup_w(vector, 0, RELU, 2)
+        regroup_w(scalar, 0, GELU)
+        regroup_w(vector, 0, SIGMOID)
+        transpose_x(0, 0, scalar)
+        transpose_x(0, 1, scalar)
+        quantise_w(0, RELU, 2)
+        quantise_w(0, SIGMOID, 2)
+        transpose_x(1, 0, scalar)
+        transpose_x(1, 1, scalar)
+        bias_columns()
+        quantise_x(0, 0, 2)
+        first_product(0, TANH, RELU, SIGMOID, GELU)
+
+        regroup_w(vector, 1, RELU, 2)
+        quantise_x(1, 0, 2)
+        regroup_w(scalar, 1, SIGMOID)
+        regroup_w(scalar, 1, GELU)
+        quantise_w(1, SIGMOID)
+        quantise_w(1, RELU, 2)
+        quantise_w(1, GELU)
+
+        first_product(1, SIGMOID, TANH, RELU, GELU)
+        stand_in(6)
+        regroup_agg(scalar, 0, 160)
+        regroup_agg(vector, 160, D_OUT)
+        sigmoid_tanh()
+        sigmoid_end(nc.gpsimd)
+        activate(TANH, ACT.Tanh)
+        activate(GELU, ACT.Gelu, 0, P)
+        activate(GELU, ACT.Gelu, P, TOKENS)
+        relu()
+        quantise_agg(0, HALF_OUT)
+        regroup_c(vector, 0, 0, 64)
+        regroup_c(scalar, 0, 64, P)
+        quantise_c(0)
+        regroup_c(scalar, 1)
+        quantise_agg(HALF_OUT, D_OUT)
+        quantise_c(1)
+        second_product(0, 0, HALF_OUT, scalar, 0)
+        second_product(0, HALF_OUT, D_OUT, vector, 1)
+        second_product(1, 0, HALF_OUT, scalar, 2)
+        second_product(1, HALF_OUT, D_OUT, vector, 3)

@@ -261,21 +261,27 @@ def tile_kan_s_kernel(tc, x, W, b, agg, out):
 
         first_product(1, SIGMOID, TANH, RELU, GELU)
         stand_in(6)
-        regroup_agg(scalar, 0, 160)
-        regroup_agg(vector, 160, D_OUT)
-        sigmoid_tanh()
-        sigmoid_end(nc.gpsimd)
-        activate(TANH, ACT.Tanh)
+        regroup_agg(scalar, 0, 64)
+        regroup_agg(vector, 64, HALF_OUT)
+        regroup_agg(vector, HALF_OUT, D_OUT)
+        sigmoid_tanh(0, P)
+        sigmoid_end(nc.gpsimd, 0, P)
+        sigmoid_tanh(P, TOKENS)
+        sigmoid_end(nc.gpsimd, P, TOKENS)
+        activate(TANH, ACT.Tanh, 0, P)
+        activate(RELU, ACT.Relu, 0, P)
         activate(GELU, ACT.Gelu, 0, P)
+        activate(TANH, ACT.Tanh, P, TOKENS)
+        activate(RELU, ACT.Relu, P, TOKENS)
         activate(GELU, ACT.Gelu, P, TOKENS)
-        relu()
+        regroup_c(vector, 0, 0, 80)
+        regroup_c(scalar, 0, 80, P)
         quantise_agg(0, HALF_OUT)
-        regroup_c(vector, 0, 0, 64)
-        regroup_c(scalar, 0, 64, P)
         quantise_c(0)
         regroup_c(scalar, 1)
         quantise_agg(HALF_OUT, D_OUT)
         quantise_c(1)
+
         second_product(0, 0, HALF_OUT, scalar, 0)
         second_product(0, HALF_OUT, D_OUT, vector, 1)
         second_product(1, 0, HALF_OUT, scalar, 2)

@@ -29,23 +29,35 @@ FLOPS = 2 * TOKENS * D_IN * BRANCHES + 2 * TOKENS * BRANCHES * D_OUT
 def tile_kan_s_kernel(tc, x, W, b, agg, out):
     nc = tc.nc
     with tc.tile_pool(name="keep", bufs=1) as keep, tc.psum_pool(name="psum", bufs=1) as psum, tc.manual_schedule():
+        zero = keep.tile([P, 1], F32)
+        nc.vector.memset(zero[:], 0.0)
+        zeros = keep.tile([P, PACK * P], BF16, align_bytes=64)
+        nc.vector.memset(zeros[:], 0.0)
         ident = keep.tile([P, P], F32)
         make_identity(nc, ident[:])
         b_rows = keep.tile([P, P], BF16)
         nc.vector.memset(b_rows[:], 0.0)
-        zero = keep.tile([P, 1], F32)
-        nc.vector.memset(zero[:], 0.0)
         half = keep.tile([P, 1], F32)
         nc.vector.memset(half[:], 0.5)
 
         warm = keep.tile([P, 1], F32)
         nc.scalar.activation(out=warm[:], in_=zero[:], func=ACT.Gelu)
+        zero_codes = keep.tile([P, P], U32, align_bytes=64)
+        zero_scales = keep.tile([P, P], U8, align_bytes=64)
+        nc.vector.quantize_mx(out=zero_codes[:].bitcast(FP8X4), scales=zero_scales[:], in_=zeros[:])
         ident_bf = keep.tile([P, P], BF16)
         nc.vector.tensor_copy(out=ident_bf[:], in_=ident[:])
 
         def bank(number, label):
             tile = psum.tile([P, BANK], F32, name=label, tag="bank%d" % number)
             return tile
+
+        early_ps = bank(7, "early_ps")
+        for n in range(15):
+            nc.tensor.matmul_mx(
+                out=early_ps[:, 0:P], lhsT=zero_codes[:].bitcast(FP8X4), lhsT_scale=zero_scales[:],
+                rhs=zero_codes[:].bitcast(FP8X4), rhs_scale=zero_scales[:], start=True, stop=True,
+            )
 
         def bank_bf16(number, label):
             tile = psum.tile([P, 2 * BANK], BF16, name=label, tag="bank%d" % number)

@@ -37,8 +37,6 @@ def tile_kan_s_kernel(tc, x, W, b, agg, out):
         make_identity(nc, ident[:])
         b_rows = keep.tile([P, P], BF16)
         nc.vector.memset(b_rows[:], 0.0)
-        half = keep.tile([P, 1], F32)
-        nc.vector.memset(half[:], 0.5)
 
         warm = keep.tile([P, 1], F32)
         nc.scalar.activation(out=warm[:], in_=zero[:], func=ACT.Gelu)
@@ -273,19 +271,16 @@ def tile_kan_s_kernel(tc, x, W, b, agg, out):
 
         first_product(1, SIGMOID, TANH, RELU, GELU)
         stand_in(6)
+
         regroup_agg(scalar, 0, 64)
-        regroup_agg(vector, 64, HALF_OUT)
-        regroup_agg(vector, HALF_OUT, D_OUT)
-        sigmoid_tanh(0, P)
-        sigmoid_end(nc.gpsimd, 0, P)
-        sigmoid_tanh(P, TOKENS)
-        sigmoid_end(nc.gpsimd, P, TOKENS)
-        activate(TANH, ACT.Tanh, 0, P)
-        activate(RELU, ACT.Relu, 0, P)
+        sigmoid_tanh()
+        activate(TANH, ACT.Tanh)
+        activate(RELU, ACT.Relu)
         activate(GELU, ACT.Gelu, 0, P)
-        activate(TANH, ACT.Tanh, P, TOKENS)
-        activate(RELU, ACT.Relu, P, TOKENS)
         activate(GELU, ACT.Gelu, P, TOKENS)
+        regroup_agg(vector, 64, HALF_OUT)
+        sigmoid_end(nc.vector)
+        regroup_agg(vector, HALF_OUT, D_OUT)
         regroup_c(vector, 0, 0, 80)
         regroup_c(scalar, 0, 80, P)
         quantise_agg(0, HALF_OUT)
@@ -293,7 +288,6 @@ def tile_kan_s_kernel(tc, x, W, b, agg, out):
         regroup_c(scalar, 1)
         quantise_agg(HALF_OUT, D_OUT)
         quantise_c(1)
-
         second_product(0, 0, HALF_OUT, scalar, 0)
         second_product(0, HALF_OUT, D_OUT, vector, 1)
         second_product(1, 0, HALF_OUT, scalar, 2)

@@ -31,10 +31,13 @@ def tile_kan_s_kernel(tc, x, W, b, agg, out):
     with tc.tile_pool(name="keep", bufs=1) as keep, tc.psum_pool(name="psum", bufs=1) as psum, tc.manual_schedule():
         zero = keep.tile([P, 1], F32)
         nc.vector.memset(zero[:], 0.0)
+        ident = keep.tile([P, P], F32)
+        nc.vector.memset(ident[:], 0.0)
+        make_identity(nc, ident[:], nomemset=True)
+        ident_bf = keep.tile([P, PACK], BF16)
+        nc.gpsimd.tensor_copy(out=ident_bf[:], in_=ident[:, 0:PACK])
         zeros = keep.tile([P, PACK * P], BF16, align_bytes=64)
         nc.vector.memset(zeros[:], 0.0)
-        ident = keep.tile([P, P], F32)
-        make_identity(nc, ident[:])
         b_rows = keep.tile([P, P], BF16)
         nc.vector.memset(b_rows[:], 0.0)
 
@@ -43,8 +46,6 @@ def tile_kan_s_kernel(tc, x, W, b, agg, out):
         zero_codes = keep.tile([P, P], U32, align_bytes=64)
         zero_scales = keep.tile([P, P], U8, align_bytes=64)
         nc.vector.quantize_mx(out=zero_codes[:].bitcast(FP8X4), scales=zero_scales[:], in_=zeros[:])
-        ident_bf = keep.tile([P, P], BF16)
-        nc.vector.tensor_copy(out=ident_bf[:], in_=ident[:])
 
         def bank(number, label):
             tile = psum.tile([P, BANK], F32, name=label, tag="bank%d" % number)
@@ -179,12 +180,6 @@ def tile_kan_s_kernel(tc, x, W, b, agg, out):
                 out=agg_grp[:, first:last, :].rearrange("p (c i) t -> p c t i", i=4),
                 in_=agg_raw[:, :, first:last].rearrange("p t (c i) -> p c t i", i=4),
             )
-
-        def interleave(number, label, dst, src):
-            n = dst.shape[1]
-            ps = bank_bf16(number, label)[:, 0 : 4 * n]
-            nc.tensor.matmul(ps.rearrange("p (c t) -> p c t", t=PACK), lhsT=ident_bf[:], rhs=src.rearrange("p t c -> p c t"), start=True, stop=True)
-            return ps
 
         def quantise_agg(first, last):
             nc.vector.quantize_mx(

from concourse import mybir
from concourse.masks import make_identity

F32 = mybir.dt.float32
BF16 = mybir.dt.bfloat16
U32 = mybir.dt.uint32
U8 = mybir.dt.uint8
FP8X4 = mybir.dt.float8_e4m3fn_x4
ACT = mybir.ActivationFunctionType
ALU = mybir.AluOpType

P = 128
PACK = 4
K_PASS = P * PACK

TOKENS = 256
D_IN = 1024
BRANCHES = 512
D_OUT = 512
TOKEN_TILES = TOKENS // P
D_PASSES = D_IN // K_PASS
RELU, TANH, SIGMOID, GELU = range(4)
HALF_OUT = D_OUT // 2
BANK = 512

FLOPS = 2 * TOKENS * D_IN * BRANCHES + 2 * TOKENS * BRANCHES * D_OUT


def tile_kan_s_kernel(tc, x, W, b, agg, out):
    nc = tc.nc
    with tc.tile_pool(name="keep", bufs=1) as keep, tc.psum_pool(name="psum", bufs=1) as psum, tc.manual_schedule():
        zero = keep.tile([P, 1], F32)
        nc.vector.memset(zero[:], 0.0)
        ident = keep.tile([P, P], F32)
        nc.vector.memset(ident[:], 0.0)
        make_identity(nc, ident[:], nomemset=True)
        ident_bf = keep.tile([P, PACK], BF16)
        nc.gpsimd.tensor_copy(out=ident_bf[:], in_=ident[:, 0:PACK])
        zeros = keep.tile([P, PACK * P], BF16, align_bytes=64)
        nc.vector.memset(zeros[:], 0.0)
        b_rows = keep.tile([P, P], BF16)
        nc.vector.memset(b_rows[:], 0.0)

        warm = keep.tile([P, 1], F32)
        nc.scalar.activation(out=warm[:], in_=zero[:], func=ACT.Gelu)
        zero_codes = keep.tile([P, P], U32, align_bytes=64)
        zero_scales = keep.tile([P, P], U8, align_bytes=64)
        nc.vector.quantize_mx(out=zero_codes[:].bitcast(FP8X4), scales=zero_scales[:], in_=zeros[:])

        def bank(number, label):
            tile = psum.tile([P, BANK], F32, name=label, tag="bank%d" % number)
            return tile

        early_ps = bank(7, "early_ps")
        for n in range(15):
            nc.tensor.matmul_mx(
                out=early_ps[:, 0:P], lhsT=zero_codes[:].bitcast(FP8X4), lhsT_scale=zero_scales[:],
                rhs=zero_codes[:].bitcast(FP8X4), rhs_scale=zero_scales[:], start=True, stop=True,
            )

        def bank_bf16(number, label):
            tile = psum.tile([P, 2 * BANK], BF16, name=label, tag="bank%d" % number)
            return tile

        x_sb = {}
        for g in range(D_PASSES):
            for i in range(TOKEN_TILES):
                x_tile = keep.tile([P, K_PASS], BF16, name="x_sb%d%d" % (g, i))
                x_sb[g, i] = x_tile
        w_raw = keep.tile([P, D_PASSES, PACK, BRANCHES], BF16)
        agg_raw = keep.tile([P, PACK, D_OUT], BF16)

        def load_x(g, i):
            nc.sync.dma_start(out=x_sb[g, i][:], in_=x[i * P : (i + 1) * P, g * K_PASS : (g + 1) * K_PASS])

        def load_b():
            nc.sync.dma_start(out=b_rows[0:PACK, :], in_=b.rearrange("(f p) -> f p", f=PACK))

        def load_w(g):
            rows = slice(g * K_PASS, (g + 1) * K_PASS)
            nc.sync.dma_start(out=w_raw[:, g, :, :], in_=W[rows, :].rearrange("(p t) c -> p t c", t=PACK))

        def load_agg():
            nc.sync.dma_start(out=agg_raw[:], in_=agg.rearrange("(t p) o -> p t o", t=PACK))

        load_w(0)
        load_x(0, 0)
        load_x(0, 1)
        load_b()
        load_x(1, 0)
        load_x(1, 1)
        load_w(1)
        load_agg()

        x_grp = keep.tile([P, D_PASSES, TOKENS, PACK], BF16, align_bytes=64)
        x_grp_words = (
            x_grp[:].rearrange("p g n t -> p (g n t)").bitcast(F32)
            .rearrange("p (g n u) -> p g n u", g=D_PASSES, u=2)
        )
        x_codes = keep.tile([P, D_PASSES, TOKENS], U32, align_bytes=64)
        x_scales = keep.tile([P, D_PASSES, TOKENS], U8, align_bytes=64)
        w_grp = keep.tile([P, D_PASSES, BRANCHES, PACK], BF16, align_bytes=64)
        w_codes = keep.tile([P, D_PASSES, BRANCHES], U32, align_bytes=64)
        w_scales = keep.tile([P, D_PASSES, BRANCHES], U8, align_bytes=64)
        agg_grp = keep.tile([P, D_OUT, PACK], BF16, align_bytes=64)
        agg_codes = keep.tile([P, D_OUT], U32, align_bytes=64)
        agg_scales = keep.tile([P, D_OUT], U8, align_bytes=64)
        act = keep.tile([P, PACK, TOKENS], BF16)
        sig = keep.tile([P, TOKENS], F32)
        c_grp = keep.tile([P, TOKEN_TILES, P, PACK], BF16, align_bytes=64)
        c_codes = keep.tile([P, TOKEN_TILES, P], U32, align_bytes=64)
        c_scales = keep.tile([P, TOKEN_TILES, P], U8, align_bytes=64)
        bias = keep.tile([P, PACK], F32)
        half_bias = keep.tile([P, 1], F32)

        scalar = nc.scalar.copy
        vector = nc.vector.tensor_copy

        def transpose_x(g, i, copy):
            words = x_sb[g, i][:].bitcast(F32)
            xt = bank(2 * g + i, "xt%d%d" % (g, i))[:, 0 : 2 * P].rearrange("p (u n) -> p u n", u=2)
            for u in range(2):
                nc.tensor.transpose(xt[:, u, :], words[:, u : 2 * P : 2], ident[:])
            copy(out=x_grp_words[:, g, i * P : (i + 1) * P, :], in_=xt.rearrange("p u n -> p n u"))

        def quantise_x(g, i, count=1):
            tokens = slice(i * P, (i + count) * P)
            nc.vector.quantize_mx(
                out=x_codes[:, g, tokens].bitcast(FP8X4),
                scales=x_scales[:, g, tokens],
                in_=x_grp[:, g, tokens, :].rearrange("p n t -> p (n t)"),
            )

        def regroup_w(copy, g, f, count=1):
            cols = slice(f * P, (f + count) * P)
            copy(
                out=w_grp[:, g, cols, :].rearrange("p (c i) t -> p c t i", i=4),
                in_=w_raw[:, g, :, cols].rearrange("p t (c i) -> p c t i", i=4),
            )

        def quantise_w(g, f, count=1):
            cols = slice(f * P, (f + count) * P)
            nc.vector.quantize_mx(
                out=w_codes[:, g, cols].bitcast(FP8X4),
                scales=w_scales[:, g, cols],
                in_=w_grp[:, g, cols, :].rearrange("p c t -> p (c t)"),
            )

        h_ps = {}

        def first_product(g, *functions):
            for f in functions:
                if g == 0:
                    h_ps[f] = bank(4 + f, "h_ps%d" % f)[:, 0:TOKENS]
                cols = slice(f * P, (f + 1) * P)
                nc.tensor.matmul_mx(
                    out=h_ps[f],
                    lhsT=w_codes[:, g, cols].bitcast(FP8X4),
                    lhsT_scale=w_scales[:, g, cols],
                    rhs=x_codes[:, g, :].bitcast(FP8X4),
                    rhs_scale=x_scales[:, g, :],
                    start=(g == 0),
                    stop=(g == D_PASSES - 1),
                )

        def bias_columns():
            bias_ps = bank(0, "bias_ps")[:, 0:PACK]
            nc.tensor.matmul(bias_ps, lhsT=b_rows[:], rhs=ident_bf[:, 0:PACK], start=True, stop=True)
            nc.scalar.copy(out=bias[:], in_=bias_ps)
            nc.scalar.mul(out=half_bias[:], in_=bias_ps[:, SIGMOID : SIGMOID + 1], mul=0.5)

        def bias_columns_v():
            bias_ps = bank(0, "bias_ps")[:, 0:PACK]
            nc.tensor.matmul(bias_ps, lhsT=b_rows[:], rhs=ident_bf[:, 0:PACK], start=True, stop=True)
            nc.vector.tensor_copy(out=bias[:], in_=bias_ps)
            nc.vector.tensor_scalar(out=half_bias[:], in0=bias_ps[:, SIGMOID : SIGMOID + 1], scalar1=0.5, scalar2=None, op0=ALU.mult)

        def regroup_agg(copy, first, last):
            copy(
                out=agg_grp[:, first:last, :].rearrange("p (c i) t -> p c t i", i=4),
                in_=agg_raw[:, :, first:last].rearrange("p t (c i) -> p c t i", i=4),
            )

        def quantise_agg(first, last):
            nc.vector.quantize_mx(
                out=agg_codes[:, first:last].bitcast(FP8X4),
                scales=agg_scales[:, first:last],
                in_=agg_grp[:, first:last, :].rearrange("p o t -> p (o t)"),
            )

        def regroup_c(copy, i, a=0, z=P):
            copy(
                out=c_grp[:, i, a:z, :].rearrange("p (c i) t -> p c t i", i=4),
                in_=act[:, :, i * P + a : i * P + z].rearrange("p t (c i) -> p c t i", i=4),
            )

        def quantise_c(i):
            nc.vector.quantize_mx(
                out=c_codes[:, i, :].bitcast(FP8X4),
                scales=c_scales[:, i, :],
                in_=c_grp[:, i, :, :].rearrange("p n t -> p (n t)"),
            )

        def sigmoid_tanh(first=0, last=TOKENS):
            nc.scalar.activation(out=sig[:, first:last], in_=h_ps[SIGMOID][:, first:last], func=ACT.Tanh, scale=0.5, bias=half_bias[:, 0:1])

        def sigmoid_end(engine, first=0, last=TOKENS):
            engine.tensor_scalar(out=act[:, SIGMOID, first:last], in0=sig[:, first:last], scalar1=0.5, scalar2=0.5, op0=ALU.mult, op1=ALU.add)

        def activate(f, func, first=0, last=TOKENS):
            nc.scalar.activation(out=act[:, f, first:last], in_=h_ps[f][:, first:last], func=func, bias=bias[:, f : f + 1])

        def relu():
            nc.vector.tensor_scalar(
                out=act[:, RELU, :], in0=h_ps[RELU], scalar1=bias[:, RELU : RELU + 1], scalar2=0.0,
                op0=ALU.add, op1=ALU.max,
            )

        def stand_in(count, first=0):
            idle_ps = bank(0, "idle_ps")
            for n in range(count):
                nc.tensor.matmul_mx(
                    out=idle_ps[:, 0:TOKENS], lhsT=w_codes[:, 1, 0:P].bitcast(FP8X4), lhsT_scale=w_scales[:, 1, 0:P],
                    rhs=x_codes[:, 1, :].bitcast(FP8X4), rhs_scale=x_scales[:, 1, :], start=True, stop=True,
                )

        out_sb = {}
        for i in range(TOKEN_TILES):
            out_tile = keep.tile([P, D_OUT], F32, name="out_sb%d" % i)
            out_sb[i] = out_tile

        def second_product(i, first, last, copy, number):
            out_ps = bank(number, "out_ps%d_%d" % (i, first))[:, 0 : last - first]
            nc.tensor.matmul_mx(
                out=out_ps,
                lhsT=c_codes[:, i, :].bitcast(FP8X4),
                lhsT_scale=c_scales[:, i, :],
                rhs=agg_codes[:, first:last].bitcast(FP8X4),
                rhs_scale=agg_scales[:, first:last],
                start=True,
                stop=True,
            )
            copy(out=out_sb[i][:, first:last], in_=out_ps)
            nc.sync.dma_start(out=out[i * P : (i + 1) * P, first:last], in_=out_sb[i][:, first:last])

        regroup_w(vector, 0, RELU, 2)
        regroup_w(scalar, 0, GELU)
        regroup_w(vector, 0, SIGMOID)
        transpose_x(0, 0, scalar)
        transpose_x(0, 1, scalar)
        quantise_w(0, RELU, 2)
        quantise_w(0, SIGMOID, 2)
        transpose_x(1, 0, scalar)
        transpose_x(1, 1, scalar)
        bias_columns()
        quantise_x(0, 0, 2)
        first_product(0, TANH, RELU, SIGMOID, GELU)

        regroup_w(vector, 1, RELU, 2)
        quantise_x(1, 0, 2)
        regroup_w(scalar, 1, SIGMOID)
        regroup_w(scalar, 1, GELU)
        quantise_w(1, SIGMOID)
        quantise_w(1, RELU, 2)
        quantise_w(1, GELU)

        first_product(1, SIGMOID, TANH, RELU, GELU)
        stand_in(6)

        regroup_agg(scalar, 0, 64)
        sigmoid_tanh()
        activate(TANH, ACT.Tanh)
        activate(RELU, ACT.Relu)
        activate(GELU, ACT.Gelu, 0, P)
        activate(GELU, ACT.Gelu, P, TOKENS)
        regroup_agg(vector, 64, HALF_OUT)
        sigmoid_end(nc.vector)
        regroup_agg(vector, HALF_OUT, D_OUT)
        regroup_c(vector, 0, 0, 80)
        regroup_c(scalar, 0, 80, P)
        quantise_agg(0, HALF_OUT)
        quantise_c(0)
        regroup_c(scalar, 1)
        quantise_agg(HALF_OUT, D_OUT)
        quantise_c(1)
        second_product(0, 0, HALF_OUT, scalar, 0)
        second_product(0, HALF_OUT, D_OUT, vector, 1)
        second_product(1, 0, HALF_OUT, scalar, 2)
        second_product(1, HALF_OUT, D_OUT, vector, 3)
